import numpy as np
import ml_dtypes


def mxq(x, axis, fmt="e4m3"):
    dtype, down = {"e4m3": (ml_dtypes.float8_e4m3fn, 7), "e5m2": (ml_dtypes.float8_e5m2, 14)}[fmt]
    v = np.moveaxis(np.asarray(x, np.float32).astype(ml_dtypes.bfloat16).astype(np.float64), axis, -1)
    blocks = v.reshape(v.shape[:-1] + (-1, 32))
    amax = np.abs(blocks).max(-1, keepdims=True)
    byte = np.maximum(np.where(amax > 0, np.frexp(amax)[1] - 1 + 127, 0) - down, 1)
    scale = np.exp2(byte - 127.0)
    codes = (blocks / scale).astype(np.float32).astype(dtype).astype(np.float64)
    return np.moveaxis((codes * scale).reshape(v.shape), -1, axis)


WIDE = False


def mx_kscale(k):
    if not WIDE:
        return np.ones(k)
    levels = np.array([30, -30])
    if k % 512:
        return np.exp2(np.random.permutation(np.resize(levels, k // 32))).repeat(32)
    a = np.empty((k // 512, 16))
    for p in range(k // 512):
        a[p, :8] = np.random.permutation(np.resize(levels, 8))
        for g in range(8):
            far = levels[np.abs(levels - a[p, g]) >= 10]
            a[p, g + 8] = far[np.random.randint(len(far))]
    return np.exp2(a.ravel()).repeat(32)


BF16 = ml_dtypes.bfloat16


def bf(x):
    return np.asarray(x, np.float32).astype(BF16)


def f64(x):
    return np.asarray(x).astype(np.float64)


E2M1 = np.array([0.0, 0.5, 1.0, 1.5, 2.0, 3.0, 4.0, 6.0, -0.0, -0.5, -1.0, -1.5, -2.0, -3.0, -4.0, -6.0])


def pack_weight(w, fmt):
    k, n = w.shape
    w = f64(bf(w)).reshape(k // 32, 32, n)
    amax = np.abs(w).max(1)
    if fmt == "e4m3":
        byte = np.frexp(amax)[1] - 1 + 127 - 7
    else:
        mant, ex = np.frexp(amax / 6.0)
        byte = np.where(mant > 0.5, ex, ex - 1) + 127
    byte = np.clip(np.where(amax > 0, byte, 1), 1, 254)
    scaled = (w * np.exp2(127.0 - byte)[:, None, :]).reshape(k, n).astype(np.float32)
    by_word = np.ascontiguousarray(scaled.reshape(k // 512, 128, 4, n).transpose(0, 1, 3, 2))
    if fmt == "e4m3":
        words = by_word.astype(ml_dtypes.float8_e4m3fn).view(np.uint8)
    else:
        c = by_word.astype(ml_dtypes.float4_e2m1fn).view(np.uint8) & 0xF
        words = c[..., 0::2] | (c[..., 1::2] << 4)
    return np.ascontiguousarray(words), np.ascontiguousarray(byte.astype(np.uint8).reshape(k // 512, 16, n))


def unpack_weight(words, scales, fmt):
    g, p, n, _ = words.shape
    if fmt == "e4m3":
        vals = np.ascontiguousarray(words).view(ml_dtypes.float8_e4m3fn).astype(np.float64)
    else:
        nib = np.empty((g, p, n, 4), np.uint8)
        nib[..., 0::2] = words & 0xF
        nib[..., 1::2] = words >> 4
        vals = E2M1[nib]
    vals = vals * np.repeat(np.exp2(scales.astype(np.float64) - 127.0), 8, axis=1)[..., None]
    return vals.transpose(0, 1, 3, 2).reshape(g * 512, n)

def pack4(w):
    words, scales = pack_weight(w, "e2m1")
    return words.reshape(words.shape[0], 128, -1), scales


def unpack4(words, scales):
    return unpack_weight(words.reshape(words.shape[0], 128, -1, 2), scales, "e2m1")


B, N, D, H, HD, S, DO = 1, 1536, 1024, 16, 64, 11, 1024
E = H * HD
D4 = [0.4829629131445341, 0.8365163037378079, 0.2241438680420134, -0.1294095225512604]
T = len(D4)


def elu1(u):
    return np.where(u > 0.0, u, np.exp(np.minimum(u, 0.0)) - 1.0) + 1.0


def softplus(u):
    return np.log(1.0 + np.exp(u))


def shifted(t, o):
    if o == 0:
        return t
    return np.concatenate([np.zeros((B, H, o, HD)), t[:, :, :N - o, :]], axis=2)


def setup_inputs():
    s = mx_kscale(D)
    lg = np.random.standard_normal((B, H, N, S)) * 1.4
    g = np.exp(lg - lg.max(-1, keepdims=True))
    x = bf(np.random.standard_normal((B, N, D)) * s)
    w = np.random.standard_normal((3 * E, D)) * 0.6 / np.sqrt(D) / s
    words, scales = pack4(w.T)
    return {"x": x,
            "W_qkv_words": words,
            "W_qkv_scales": scales,
            "b_qkv": bf(np.random.standard_normal(3 * E) * 0.1),
            "gains": bf(g / g.sum(-1, keepdims=True)),
            "pos_bias": bf(np.random.standard_normal((S * T, H)) * 0.5),
            "identity_bypass": bf(-1.0 + 0.5 * np.random.standard_normal(H))}


def reference(x, W_qkv_words, W_qkv_scales, b_qkv, gains, pos_bias, identity_bypass):
    qkv = (mxq(f64(x), 2, "e5m2") @ unpack4(W_qkv_words, W_qkv_scales)) + f64(b_qkv)
    q, k, v = [t.reshape(B, N, H, HD).transpose(0, 2, 1, 3) for t in np.split(qkv, 3, axis=-1)]
    g, pb = f64(gains), f64(pos_bias)
    acc = np.zeros((B, H, N, HD))
    z = np.zeros((B, H, N, 1))
    tap = 0
    for j in range(S):
        d = 1 << j
        g_j = g[..., j][..., None]
        for tau, c in enumerate(D4):
            o = d * tau
            bias = pb[tap].reshape(1, H, 1, 1)
            tap += 1
            if o != 0 and o >= N:
                continue
            k_s, v_s = shifted(k, o), shifted(v, o)
            feat = elu1(np.sum(q * k_s, -1, keepdims=True) + bias)
            acc = acc + (g_j * c) * feat * v_s
            z = z + g_j * abs(c) * feat
    p = softplus(f64(identity_bypass)).reshape(1, H, 1, 1)
    local = elu1(np.sum(q * k, -1, keepdims=True))
    acc = acc + p * local * v
    z = z + p * local
    res = acc / (z + 1e-06)
    return res.transpose(0, 2, 1, 3).reshape(B, N, E)

@@ -1,0 +1,439 @@
+from contextlib import ExitStack
+
+import concourse.mybir as mybir
+from concourse.masks import make_identity
+
+N, D, H, HD, S = 1536, 1024, 16, 64, 11
+E = H * HD
+D4 = [0.4829629131445341, 0.8365163037378079, 0.2241438680420134, -0.1294095225512604]
+FLOPS = 2 * N * D * 3 * E
+
+F32 = mybir.dt.float32
+BF16 = mybir.dt.bfloat16
+I32 = mybir.dt.int32
+U32 = mybir.dt.uint32
+U8 = mybir.dt.uint8
+E5M2X4 = mybir.dt.float8_e5m2_x4
+E2M1X4 = mybir.dt.float4_e2m1fn_x4
+ALU = mybir.AluOpType
+ACT = mybir.ActivationFunctionType
+AXIS = mybir.AxisListType
+
+P = 128
+TILES = N // P
+PASSES = D // 512
+CHUNKS = 8
+LANES = HD // CHUNKS
+BANK = 4
+PAD = 96
+OFFSETS = sorted({(1 << j) * tau for j in range(S) for tau in range(4) if (1 << j) * tau < N})
+SLOTS = len(OFFSETS)
+ZERO_TAPS = 1 + S
+TAPS = 42
+LAG = 2
+WEIGHT_WORK = 6
+
+
+def live_slots(t):
+    return [s for s in range(SLOTS) if OFFSETS[s] < P * (t + 1)]
+
+
+def slot_groups(t):
+    live = live_slots(t)
+    return [live[i : i + BANK] for i in range(0, len(live), BANK)]
+
+
+def on_gpsimd(i, share):
+    return (i + 1) * share[0] // share[1] > i * share[0] // share[1]
+
+
+def tile_dwarfattention_pa_kernel(tc, x, W_qkv_words, W_qkv_scales, b_qkv, gains, pos_bias, identity_bypass, out):
+    nc = tc.nc
+    with ExitStack() as ctx:
+        ctx.enter_context(tc.manual_schedule())
+        keep = ctx.enter_context(tc.tile_pool(name="keep", bufs=1))
+        psum = ctx.enter_context(tc.psum_pool(name="psum", bufs=2))
+
+        ident = keep.tile([P, P], F32)
+        ident_bf = keep.tile([P, P], BF16)
+        kT = keep.tile([P, CHUNKS, PAD + N], F32)
+        vT = keep.tile([P, CHUNKS, PAD + N], F32)
+        w_codes = [keep.tile([P, PASSES, 2 * E], U8, name="w_codes%d" % i, align_bytes=64) for i in range(3)]
+        w_scales = [keep.tile([P, PASSES, E], U8, name="w_scales%d" % i, align_bytes=64) for i in range(3)]
+        x_codes = keep.tile([P, TILES, PASSES * P], U32, align_bytes=64)
+        x_scales = keep.tile([P, TILES, PASSES * P], U8, align_bytes=64)
+        gain = keep.tile([P, S, H * TILES], BF16)
+        bias = keep.tile([P, 3 * CHUNKS], F32)
+        tap_bias = keep.tile([P, TAPS, H], F32)
+        tap_gain = keep.tile([P, TAPS, H], F32)
+
+        with tc.tile_pool(name="head", bufs=1) as head:
+            scale_rows = head.tile([P, PASSES, 3 * E], U8)
+            bias_rows = head.tile([P, P], BF16)
+            nc.vector.memset(scale_rows[:].bitcast(I32), 0)
+            nc.vector.memset(bias_rows[:], 0.0)
+            make_identity(nc, ident[:])
+            make_identity(nc, ident_bf[:])
+            nc.gpsimd.memset(kT[:, :, 0:PAD], 0.0)
+            nc.gpsimd.memset(vT[:, :, 0:PAD], 0.0)
+
+            x_rows = {}
+
+            def load_x(t):
+                x_rows[t] = head.tile([P, D], BF16, name="x_rows", bufs=TILES)
+                nc.sync.dma_start(out=x_rows[t][:], in_=x[0, t * P : (t + 1) * P, :])
+
+            words = [head.tile([P, PASSES, 2 * E], U8, name="words%d" % i) for i in range(3)]
+            bypass = head.tile([P, H], BF16)
+            pos = head.tile([P, S, 4, H], BF16)
+            gain_rows = [head.tile([P, P * S], BF16, name="gain_rows%d" % i) for i in range(2)]
+
+            def load_words(i):
+                src = W_qkv_words[:, :, 2 * E * i : 2 * E * (i + 1)].rearrange("g p n -> p g n")
+                nc.sync.dma_start(out=words[i][:].bitcast(I32), in_=src.bitcast(I32))
+
+            nc.sync.dma_start(out=bypass[:], in_=identity_bypass.partition_broadcast(P))
+            load_x(0)
+            load_words(0)
+            for quad in range(4):
+                src = W_qkv_scales[:, 4 * quad : 4 * quad + 4, :].rearrange("g r n -> r g n")
+                nc.sync.dma_start(out=scale_rows[32 * quad : 32 * quad + 4, :, :].bitcast(I32), in_=src.bitcast(I32))
+            for i in range(3):
+                nc.sync.dma_start(
+                    out=bias_rows[CHUNKS * i : CHUNKS * (i + 1), :].rearrange("c (h l) -> c h l", h=H),
+                    in_=b_qkv[E * i : E * (i + 1)].rearrange("(h c l) -> c h l", h=H, c=CHUNKS),
+                )
+            load_words(1)
+            for t in range(1, TILES):
+                load_x(t)
+            load_words(2)
+            nc.sync.dma_start(
+                out=pos[:].rearrange("p j a h -> p (j a h)"),
+                in_=pos_bias.rearrange("r h -> (r h)").partition_broadcast(P),
+            )
+            all_gain_rows = gains[0].rearrange("h (t p) j -> (h t) (p j)", p=P)
+            rows = H * TILES
+            nc.sync.dma_start(out=gain_rows[0][:], in_=all_gain_rows[0:P, :])
+            nc.sync.dma_start(out=gain_rows[1][:], in_=all_gain_rows[rows - P : rows, :])
+
+            grouped = {}
+
+            def turn_x(t):
+                xt = psum.tile([P, PASSES, 2, P], F32, tag="s", name="xt")
+                pairs = x_rows[t][:].bitcast(F32)
+                for g in range(PASSES):
+                    for u in range(2):
+                        nc.tensor.transpose(xt[:, g, u, :], pairs[:, 256 * g + u : 256 * (g + 1) : 2], ident[:])
+                grouped[t] = head.tile([P, D], BF16, name="grouped", bufs=3, align_bytes=64)
+                nc.scalar.copy(
+                    out=grouped[t][:].bitcast(F32).rearrange("p (g r u) -> p g r u", g=PASSES, u=2),
+                    in_=xt[:].rearrange("p g u r -> p g r u"),
+                )
+
+            def quantize_x(t):
+                nc.vector.quantize_mx(out=x_codes[:, t, :].bitcast(E5M2X4), scales=x_scales[:, t, :], in_=grouped[t][:])
+
+            def order_columns(i):
+                for g in range(PASSES):
+                    nc.vector.tensor_copy(
+                        out=w_codes[i][:, g, :].bitcast(I32).rearrange("p (c h w) -> p c h w", c=CHUNKS, h=H),
+                        in_=words[i][:, g, :].bitcast(I32).rearrange("p (h c w) -> p c h w", c=CHUNKS, h=H),
+                    )
+                for g in range(PASSES):
+                    nc.vector.tensor_copy(
+                        out=w_scales[i][:, g, :].bitcast(I32).rearrange("p (c h w) -> p c h w", c=CHUNKS, h=H),
+                        in_=scale_rows[:, g, E * i : E * (i + 1)].bitcast(I32).rearrange("p (h c w) -> p c h w", c=CHUNKS, h=H),
+                    )
+
+            soft = head.tile([P, 4, H], F32)
+            nc.scalar.activation(out=soft[:, 0, :], in_=bypass[:], func=ACT.Abs)
+            nc.scalar.activation(out=soft[:, 1, :], in_=soft[:, 0, :], func=ACT.Exp, scale=-1.0)
+            nc.scalar.activation(out=soft[:, 2, :], in_=soft[:, 1, :], func=ACT.Ln, bias=1.0)
+            nc.scalar.activation(out=soft[:, 3, :], in_=bypass[:], func=ACT.Relu)
+
+            turn_x(0)
+            bias_t = psum.tile([P, P], BF16, tag="w", name="bias_t")
+            nc.tensor.transpose(bias_t[:], bias_rows[:], ident_bf[:])
+            order_columns(0)
+            quantize_x(0)
+            order_columns(1)
+            nc.vector.tensor_copy(out=bias[:], in_=bias_t[:, 0 : 3 * CHUNKS])
+            nc.vector.tensor_tensor(out=tap_gain[:, 0, :], in0=soft[:, 2, :], in1=soft[:, 3, :], op=ALU.add)
+            turn_x(1)
+            for t in range(1, TILES):
+                if t + 1 < TILES:
+                    turn_x(t + 1)
+                quantize_x(t)
+            order_columns(2)
+            nc.vector.memset(tap_bias[:, 0, :], 0.0)
+            nc.vector.tensor_copy(out=tap_bias[:, 1:12, :], in_=pos[:, :, 0, :])
+            nc.vector.tensor_copy(out=tap_bias[:, 12:13, :], in_=pos[:, 0:1, 1, :])
+            nc.vector.tensor_copy(out=tap_bias[:, 13:32:2, :], in_=pos[:, 1:11, 1, :])
+            nc.vector.tensor_copy(out=tap_bias[:, 14:32:2, :], in_=pos[:, 0:9, 3, :])
+            nc.vector.tensor_copy(out=tap_bias[:, 32:42, :], in_=pos[:, 0:10, 2, :])
+            for i in range(2):
+                first = 0 if i == 0 else 2 * P - rows
+                for j0 in range(0, S, 8):
+                    count = min(8, S - j0)
+                    gain_t = psum.tile([P, 8, P], BF16, tag="w", name="gain_t")
+                    for j in range(count):
+                        nc.tensor.transpose(gain_t[:, j, :], gain_rows[i][:, j0 + j : P * S : S], ident_bf[:])
+                    nc.scalar.copy(
+                        out=gain[:, j0 : j0 + count, i * P : i * P + P - first], in_=gain_t[:, 0:count, first:P]
+                    )
+
+        work = ctx.enter_context(tc.tile_pool(name="work", bufs=1))
+        waiting = []
+
+        def later(steps, call):
+            waiting.append([steps, call])
+
+        def step():
+            for entry in waiting:
+                entry[0] -= 1
+            due = [entry for entry in waiting if entry[0] <= 0]
+            for entry in due:
+                waiting.remove(entry)
+                entry[1]()
+
+        def project(i, t, b, tag, dest):
+            acc = psum.tile([P, BANK, P], F32, tag=tag, name="proj")
+            for c in range(BANK * b, BANK * (b + 1)):
+                for g in range(PASSES):
+                    nc.tensor.matmul_mx(
+                        out=acc[:, c % BANK, :],
+                        lhsT=w_codes[i][:, g, 2 * P * c : 2 * P * (c + 1)].bitcast(E2M1X4),
+                        lhsT_scale=w_scales[i][:, g, P * c : P * (c + 1)],
+                        rhs=x_codes[:, t, P * g : P * (g + 1)].bitcast(E5M2X4),
+                        rhs_scale=x_scales[:, t, P * g : P * (g + 1)],
+                        start=(g == 0),
+                        stop=(g == PASSES - 1),
+                    )
+            for c in range(BANK * b, BANK * (b + 1)):
+                col = CHUNKS * i + c
+                nc.scalar.activation(
+                    out=dest[:, c, :], in_=acc[:, c % BANK, :], func=ACT.Identity, bias=bias[:, col : col + 1]
+                )
+            return acc
+
+        q_psum, q_sbuf, scores, weights, spread, turned, turned_sbuf = {}, {}, {}, {}, {}, {}, {}
+
+        def project_q(t, b):
+            if b == 0:
+                q_sbuf[t] = work.tile([P, CHUNKS, P], F32, name="q_sbuf", bufs=2)
+            q_psum[t, b] = project(0, t, b, "q", q_sbuf[t])
+
+        def project_k(t, b, tag):
+            project(1, t, b, tag, kT[:, :, PAD + t * P : PAD + (t + 1) * P])
+
+        def project_v(t, b, tag):
+            project(2, t, b, tag, vT[:, :, PAD + t * P : PAD + (t + 1) * P])
+
+        def product_tile(gpsimd):
+            if gpsimd:
+                return work.tile([P, CHUNKS, P], F32, name="product_g", bufs=3)
+            return work.tile([P, CHUNKS, P], F32, name="product_v", bufs=4)
+
+        def window(t, s):
+            first = PAD + t * P - OFFSETS[s]
+            return slice(first, first + P)
+
+        def gains_of_taps(t):
+            g = gain[:, :, t : H * TILES : TILES]
+            for tau, tap_rows, scales in (
+                (0, slice(1, 12), slice(0, 11)),
+                (1, slice(12, 13), slice(0, 1)),
+                (1, slice(13, 32, 2), slice(1, 11)),
+                (3, slice(14, 32, 2), slice(0, 9)),
+                (2, slice(32, 42), slice(0, 10)),
+            ):
+                nc.scalar.activation(out=tap_gain[:, tap_rows, :], in_=g[:, scales, :], func=ACT.Copy, scale=abs(D4[tau]))
+
+        def sum_lanes(t, group, part):
+            nc.vector.tensor_reduce(
+                out=scores[t][:, group[0] : group[-1] + 1, :],
+                in_=part[:, 0 : len(group), :].rearrange("p s (h l) -> p s h l", l=LANES),
+                axis=AXIS.X,
+                op=ALU.add,
+            )
+
+        parts, sums = {}, {}
+
+        def add_turned(dest, product, c, start, stop):
+            nc.tensor.matmul(dest, lhsT=product[:, c, :], rhs=ident[:], start=start, stop=stop, is_transpose=True)
+
+        def score(t, s, gpsimd):
+            group = slot_groups(t)[s // BANK]
+            if s == group[0]:
+                parts[t, s // BANK] = psum.tile([P, BANK, P], F32, tag="s", name="part")
+            part = parts[t, s // BANK]
+            product = product_tile(gpsimd)
+            keys = kT[:, :, window(t, s)]
+            if gpsimd:
+                nc.gpsimd.tensor_tensor(out=product[:], in0=q_sbuf[t][:], in1=keys, op=ALU.mult)
+            else:
+                for c in range(CHUNKS):
+                    nc.vector.scalar_tensor_tensor(
+                        out=product[:, c, :],
+                        in0=q_psum[t, c // BANK][:, c % BANK, :],
+                        scalar=bias[:, c : c + 1],
+                        in1=keys[:, c, :],
+                        op0=ALU.add,
+                        op1=ALU.mult,
+                    )
+            for c in range(CHUNKS):
+                add_turned(part[:, s % BANK, :], product, c, c == 0, c == CHUNKS - 1)
+            if s == group[-1]:
+                later(3, lambda: sum_lanes(t, group, part))
+
+        def weight_steps(t):
+            u = work.tile([P, TAPS, H], F32, name="u")
+            low = work.tile([P, TAPS, H], F32, name="low")
+            high = work.tile([P, TAPS, H], F32, name="high")
+            zero_taps = work.tile([P, ZERO_TAPS, H], F32, name="zero_taps")
+            rest = work.tile([P, TAPS - ZERO_TAPS + 1, H], F32, name="rest")
+            z = work.tile([P, H], F32, name="z")
+            z_eps = work.tile([P, H], F32, name="z_eps")
+            inv = work.tile([P, H], F32, name="inv")
+            weights[t] = work.tile([P, SLOTS, H], F32, name="weights", bufs=2)
+            sc = scores[t]
+
+            def add_bias():
+                nc.gpsimd.tensor_tensor(
+                    out=u[:, 0:12, :], in0=sc[:, 0:1, :].to_broadcast([P, 12, H]), in1=tap_bias[:, 0:12, :], op=ALU.add
+                )
+                nc.gpsimd.tensor_tensor(out=u[:, 12:32, :], in0=sc[:, 1:21, :], in1=tap_bias[:, 12:32, :], op=ALU.add)
+                nc.gpsimd.tensor_tensor(out=u[:, 32:42, :], in0=sc[:, 2:21:2, :], in1=tap_bias[:, 32:42, :], op=ALU.add)
+                nc.scalar.activation(out=low[:], in_=u[:], func=ACT.Relu, scale=-1.0)
+                nc.scalar.activation(out=low[:], in_=low[:], func=ACT.Exp, scale=-1.0)
+                nc.scalar.activation(out=high[:], in_=u[:], func=ACT.Relu)
+
+            def weigh():
+                nc.gpsimd.tensor_tensor(out=u[:], in0=low[:], in1=high[:], op=ALU.add)
+                nc.gpsimd.tensor_tensor(out=zero_taps[:], in0=u[:, 0:12, :], in1=tap_gain[:, 0:12, :], op=ALU.mult)
+                nc.gpsimd.tensor_tensor(out=rest[:, 1:31, :], in0=u[:, 12:42, :], in1=tap_gain[:, 12:42, :], op=ALU.mult)
+                nc.gpsimd.tensor_tensor(out=rest[:, 2:21:2, :], in0=rest[:, 2:21:2, :], in1=rest[:, 21:31, :], op=ALU.add)
+
+            def sum_zero_taps():
+                nc.vector.tensor_reduce(
+                    out=rest[:, 0, :], in_=zero_taps[:].rearrange("p r h -> p h r"), axis=AXIS.X, op=ALU.add
+                )
+
+            def sum_all():
+                nc.vector.tensor_reduce(
+                    out=z[:], in_=rest[:, 0:SLOTS, :].rearrange("p r h -> p h r"), axis=AXIS.X, op=ALU.add
+                )
+                nc.scalar.activation(out=z_eps[:], in_=z[:], func=ACT.Copy, bias=1e-06)
+
+            def invert():
+                nc.vector.reciprocal(out=inv[:], in_=z_eps[:])
+
+            def normalise():
+                nc.gpsimd.tensor_tensor(
+                    out=weights[t][:],
+                    in0=rest[:, 0:SLOTS, :],
+                    in1=inv[:].unsqueeze(1).to_broadcast([P, SLOTS, H]),
+                    op=ALU.mult,
+                )
+
+            return [(0.2, add_bias), (0.4, weigh), (0.65, sum_zero_taps), (0.7, sum_all), (0.75, invert), (0.95, normalise)]
+
+        def spread_weights(t):
+            spread[t] = work.tile([P, SLOTS, H, LANES], F32, name="spread")
+            top = len(live_slots(t))
+            for slots, sign in ((slice(0, 2), 1.0), (slice(2, top, 2), 1.0), (slice(3, top, 2), -1.0)):
+                dest = spread[t][:, slots, :, :]
+                src = weights[t][:, slots, :].unsqueeze(3).to_broadcast(list(dest.shape))
+                nc.scalar.activation(out=dest, in_=src, func=ACT.Copy, scale=sign)
+
+        def turn_weights(t, n, shared):
+            group = slot_groups(t)[n]
+            bank = psum.tile([P, BANK, P], F32, tag="w", name="turned")
+            for s in group:
+                nc.tensor.transpose(bank[:, s % BANK, :], spread[t][:, s, :, :].rearrange("p h l -> p (h l)"), ident[:])
+                turned[t, s] = bank[:, s % BANK : s % BANK + 1, :]
+            for s in group:
+                if s in shared:
+                    turned_sbuf[t, s] = work.tile([P, 1, P], F32, name="turned_sbuf", bufs=4)
+                    nc.scalar.copy(out=turned_sbuf[t, s][:], in_=turned[t, s])
+
+        def store(t):
+            result = work.tile([P, H, CHUNKS, LANES], F32, name="result", bufs=2)
+            for b in range(2):
+                nc.scalar.copy(
+                    out=result[:, :, BANK * b : BANK * (b + 1), :],
+                    in_=sums[t][b][:].rearrange("p c (h l) -> p h c l", l=LANES),
+                )
+            nc.sync.dma_start(out=out[0, t * P : (t + 1) * P, :], in_=result[:].rearrange("p h c l -> p (h c l)"))
+
+        def weigh_values(t, s, shared):
+            last = len(live_slots(t)) - 1
+            if s == 0:
+                sums[t] = [psum.tile([P, BANK, P], F32, tag="acc", name="acc") for b in range(2)]
+            product = product_tile(s in shared)
+            values = vT[:, :, window(t, s)]
+            if s in shared:
+                w = turned_sbuf[t, s][:].to_broadcast([P, CHUNKS, P])
+                nc.gpsimd.tensor_tensor(out=product[:], in0=values, in1=w, op=ALU.mult)
+            else:
+                w = turned[t, s].to_broadcast([P, CHUNKS, P])
+                nc.vector.tensor_tensor(out=product[:], in0=values, in1=w, op=ALU.mult)
+            for c in range(CHUNKS):
+                first, final = s == 0 and c % BANK == 0, s == last and c % BANK == BANK - 1
+                add_turned(sums[t][c // BANK][:, c % BANK, :], product, c, first, final)
+            if s % BANK == BANK - 1 and s // BANK + 2 <= last // BANK:
+                turn_weights(t, s // BANK + 2, shared)
+            if s == last:
+                store(t)
+
+        for b in range(2):
+            project_q(0, b)
+            project_k(0, b, "s")
+        for period in range(TILES + LAG):
+            t, tw, tv = period, period - 1, period - LAG
+            n_score = len(live_slots(t)) if t < TILES else 0
+            n_value = len(live_slots(tv)) if tv >= 0 else 0
+            total = n_score + n_value
+            side = (n_score + BANK - 1) // BANK / 2 - (WEIGHT_WORK if 0 <= tw < TILES else 0)
+            n_gpsimd = round((total + side) / 3)
+            flags = [on_gpsimd(i, (n_gpsimd, total)) for i in range(total)]
+            n_vector_scores = n_score - n_gpsimd
+            shared = [i for i in range(total) if flags[i]] if n_score == 0 else []
+            if n_score:
+                scores[t] = work.tile([P, SLOTS, H], F32, name="scores", bufs=2)
+                if n_score < SLOTS:
+                    nc.gpsimd.memset(scores[t][:, n_score:SLOTS, :], 0.0)
+            if 0 <= tw < TILES:
+                later(1, lambda tw=tw: gains_of_taps(tw))
+                for place, call in weight_steps(tw):
+                    later(max(4, round(place * total)), call)
+            if n_value:
+                spread_weights(tv)
+                later(3 if n_score else 0, lambda tv=tv, shared=shared: turn_weights(tv, 0, shared))
+                later(5 if n_score else 0, lambda tv=tv, shared=shared: turn_weights(tv, 1, shared))
+                if not n_score:
+                    step()
+            if t + 1 < TILES and not n_value:
+                for b in range(2):
+                    later(2 + 2 * b, lambda t=t, b=b: project_k(t + 1, b, "w"))
+                    later(6 + 2 * b, lambda t=t, b=b: project_v(t, b, "w"))
+            next_score = next_value = vector_done = 0
+            for i in range(total):
+                if n_score and (flags[i] or vector_done < n_vector_scores):
+                    score(t, next_score, flags[i])
+                    next_score += 1
+                    vector_done += not flags[i]
+                    if vector_done == n_vector_scores and not flags[i]:
+                        if n_value:
+                            for b in range(2):
+                                later(1 + 2 * b, lambda t=t, b=b: project_v(t, b, "q"))
+                                if t + 1 < TILES:
+                                    later(5 + 2 * b, lambda t=t, b=b: project_k(t + 1, b, "q"))
+                                    later(9 + 2 * b, lambda t=t, b=b: project_q(t + 1, b))
+                        else:
+                            project_q(t + 1, 0)
+                            project_q(t + 1, 1)
+                else:
+                    weigh_values(tv, next_value, shared)
+                    next_value += 1
+                step()

@@ -23,19 +23,47 @@ P = 128
 TILES = N // P
 PASSES = D // 512
 CHUNKS = 8
-LANES = HD // CHUNKS
 BANK = 4
-PAD = 96
+LANES = HD // CHUNKS
+V_LANES = HD // BANK
+HALF = H // 2
+QUARTER = H // 4
+K_PAD = 96
+V_PAD = 64
 OFFSETS = sorted({(1 << j) * tau for j in range(S) for tau in range(4) if (1 << j) * tau < N})
 SLOTS = len(OFFSETS)
-ZERO_TAPS = 1 + S
-TAPS = 42
+NEAR = 15
+FAR = SLOTS - NEAR
+ROW = 136
+PITCH = 264
+HEAD_WORDS = P * PITCH
 LAG = 2
 WEIGHT_WORK = 6
+PRESUM = 0
+
+ZERO_TAPS = 1 + S
+NEAR_TAPS = 33
+TAPS = 42
+TAP_RUNS = (
+    (slice(1, 12), 0, slice(0, 11)),
+    (slice(12, 13), 1, slice(0, 1)),
+    (slice(13, 26, 2), 1, slice(1, 8)),
+    (slice(14, 26, 2), 3, slice(0, 6)),
+    (slice(26, 33), 2, slice(0, 7)),
+    (slice(33, 36), 2, slice(7, 10)),
+    (slice(36, 42, 2), 3, slice(6, 9)),
+    (slice(37, 42, 2), 1, slice(8, 11)),
+)
+FAR_ROW = 25
+NEAR_SUM_ROW = FAR_ROW + FAR
 
 
 def live_slots(t):
     return [s for s in range(SLOTS) if OFFSETS[s] < P * (t + 1)]
+
+
+def far_slots(t):
+    return live_slots(t)[NEAR:]
 
 
 def slot_groups(t):
@@ -43,8 +71,8 @@ def slot_groups(t):
     return [live[i : i + BANK] for i in range(0, len(live), BANK)]
 
 
-def on_gpsimd(i, share):
-    return (i + 1) * share[0] // share[1] > i * share[0] // share[1]
+def spread_evenly(i, count, total):
+    return (i + 1) * count // total > i * count // total
 
 
 def tile_dwarfattention_pa_kernel(tc, x, W_qkv_words, W_qkv_scales, b_qkv, gains, pos_bias, identity_bypass, out):
@@ -52,137 +80,143 @@ def tile_dwarfattention_pa_kernel(tc, x, W_qkv_words, W_qkv_scales, b_qkv, gains
     with ExitStack() as ctx:
         ctx.enter_context(tc.manual_schedule())
         keep = ctx.enter_context(tc.tile_pool(name="keep", bufs=1))
+        work = ctx.enter_context(tc.tile_pool(name="work", bufs=1))
         psum = ctx.enter_context(tc.psum_pool(name="psum", bufs=2))
 
-        ident = keep.tile([P, P], F32)
+        rotations = keep.tile([P, 2 * P - H], F32)
+        ident = rotations[:, 0:P]
         ident_bf = keep.tile([P, P], BF16)
-        kT = keep.tile([P, CHUNKS, PAD + N], F32)
-        vT = keep.tile([P, CHUNKS, PAD + N], F32)
+        kT = keep.tile([P, CHUNKS, K_PAD + N], F32)
+        vT = keep.tile([P, CHUNKS, V_PAD + N], F32)
         w_codes = [keep.tile([P, PASSES, 2 * E], U8, name="w_codes%d" % i, align_bytes=64) for i in range(3)]
         w_scales = [keep.tile([P, PASSES, E], U8, name="w_scales%d" % i, align_bytes=64) for i in range(3)]
-        x_codes = keep.tile([P, TILES, PASSES * P], U32, align_bytes=64)
-        x_scales = keep.tile([P, TILES, PASSES * P], U8, align_bytes=64)
         gain = keep.tile([P, S, H * TILES], BF16)
         bias = keep.tile([P, 3 * CHUNKS], F32)
-        tap_bias = keep.tile([P, TAPS, H], F32)
+        tap_bias = keep.tile([P, TAPS, H], BF16)
         tap_gain = keep.tile([P, TAPS, H], F32)
+        by_key = keep.tile([P, H, ROW], F32)
+        bias_rows = keep.tile([P, P], BF16)
+        bypass = keep.tile([P, H], BF16)
+        soft = keep.tile([P, 4, H], F32)
 
-        with tc.tile_pool(name="head", bufs=1) as head:
-            scale_rows = head.tile([P, PASSES, 3 * E], U8)
-            bias_rows = head.tile([P, P], BF16)
-            nc.vector.memset(scale_rows[:].bitcast(I32), 0)
-            nc.vector.memset(bias_rows[:], 0.0)
-            make_identity(nc, ident[:])
-            make_identity(nc, ident_bf[:])
-            nc.gpsimd.memset(kT[:, :, 0:PAD], 0.0)
-            nc.gpsimd.memset(vT[:, :, 0:PAD], 0.0)
+        flat_out = out.rearrange("b n e -> (b n e)")
+        first_word = N * E - H * HEAD_WORDS
+        first_parked_tile = first_word // (P * E)
 
-            x_rows = {}
+        def scratch(q, pitch):
+            lo = first_word + q * QUARTER * HEAD_WORDS
+            heads = flat_out[lo : lo + QUARTER * HEAD_WORDS].rearrange("(h r) -> h r", h=QUARTER)
+            return heads[:, 0 : P * pitch].rearrange("h (m i) -> m h i", i=pitch)
 
-            def load_x(t):
-                x_rows[t] = head.tile([P, D], BF16, name="x_rows", bufs=TILES)
-                nc.sync.dma_start(out=x_rows[t][:], in_=x[0, t * P : (t + 1) * P, :])
+        x_rows, grouped, x_codes, x_scales = {}, {}, {}, {}
 
-            words = [head.tile([P, PASSES, 2 * E], U8, name="words%d" % i) for i in range(3)]
-            bypass = head.tile([P, H], BF16)
-            pos = head.tile([P, S, 4, H], BF16)
-            gain_rows = [head.tile([P, P * S], BF16, name="gain_rows%d" % i) for i in range(2)]
+        def load_x(t):
+            x_rows[t] = work.tile([P, D], BF16, name="x_rows", bufs=2)
+            nc.sync.dma_start(out=x_rows[t][:], in_=x[0, t * P : (t + 1) * P, :])
 
-            def load_words(i):
-                src = W_qkv_words[:, :, 2 * E * i : 2 * E * (i + 1)].rearrange("g p n -> p g n")
-                nc.sync.dma_start(out=words[i][:].bitcast(I32), in_=src.bitcast(I32))
-
-            nc.sync.dma_start(out=bypass[:], in_=identity_bypass.partition_broadcast(P))
-            load_x(0)
-            load_words(0)
-            for quad in range(4):
-                src = W_qkv_scales[:, 4 * quad : 4 * quad + 4, :].rearrange("g r n -> r g n")
-                nc.sync.dma_start(out=scale_rows[32 * quad : 32 * quad + 4, :, :].bitcast(I32), in_=src.bitcast(I32))
-            for i in range(3):
-                nc.sync.dma_start(
-                    out=bias_rows[CHUNKS * i : CHUNKS * (i + 1), :].rearrange("c (h l) -> c h l", h=H),
-                    in_=b_qkv[E * i : E * (i + 1)].rearrange("(h c l) -> c h l", h=H, c=CHUNKS),
-                )
-            load_words(1)
-            for t in range(1, TILES):
-                load_x(t)
-            load_words(2)
-            nc.sync.dma_start(
-                out=pos[:].rearrange("p j a h -> p (j a h)"),
-                in_=pos_bias.rearrange("r h -> (r h)").partition_broadcast(P),
+        def turn_x(t):
+            xt = psum.tile([P, PASSES, 2, P], F32, tag="w", name="xt")
+            pairs_of_k = x_rows[t][:].bitcast(F32)
+            for g in range(PASSES):
+                for u in range(2):
+                    nc.tensor.transpose(xt[:, g, u, :], pairs_of_k[:, 256 * g + u : 256 * (g + 1) : 2], ident)
+            grouped[t] = work.tile([P, D], BF16, name="grouped", align_bytes=64)
+            nc.scalar.copy(
+                out=grouped[t][:].bitcast(F32).rearrange("p (g r u) -> p g r u", g=PASSES, u=2),
+                in_=xt[:].rearrange("p g u r -> p g r u"),
             )
-            all_gain_rows = gains[0].rearrange("h (t p) j -> (h t) (p j)", p=P)
-            rows = H * TILES
-            nc.sync.dma_start(out=gain_rows[0][:], in_=all_gain_rows[0:P, :])
-            nc.sync.dma_start(out=gain_rows[1][:], in_=all_gain_rows[rows - P : rows, :])
 
-            grouped = {}
+        def quantize_x(t):
+            x_codes[t] = work.tile([P, PASSES * P], U32, name="x_codes", bufs=2, align_bytes=64)
+            x_scales[t] = work.tile([P, PASSES * P], U8, name="x_scales", bufs=2, align_bytes=64)
+            nc.vector.quantize_mx(out=x_codes[t][:].bitcast(E5M2X4), scales=x_scales[t][:], in_=grouped[t][:])
 
-            def turn_x(t):
-                xt = psum.tile([P, PASSES, 2, P], F32, tag="s", name="xt")
-                pairs = x_rows[t][:].bitcast(F32)
-                for g in range(PASSES):
-                    for u in range(2):
-                        nc.tensor.transpose(xt[:, g, u, :], pairs[:, 256 * g + u : 256 * (g + 1) : 2], ident[:])
-                grouped[t] = head.tile([P, D], BF16, name="grouped", bufs=3, align_bytes=64)
-                nc.scalar.copy(
-                    out=grouped[t][:].bitcast(F32).rearrange("p (g r u) -> p g r u", g=PASSES, u=2),
-                    in_=xt[:].rearrange("p g u r -> p g r u"),
-                )
+        scale_rows = work.tile([P, PASSES, 3 * E], U8, tag="spread")
+        words = [work.tile([P, PASSES, 2 * E], U8, name="words", tag=tag, bufs=2) for tag in ("result", "result", "v_rows")]
+        gain_rows = [work.tile([P, P * S], BF16, name="gain_rows", tag=tag) for tag in ("u", "low")]
+        pos = work.tile([P, S, 4, H], BF16, tag="weights", bufs=2)
 
-            def quantize_x(t):
-                nc.vector.quantize_mx(out=x_codes[:, t, :].bitcast(E5M2X4), scales=x_scales[:, t, :], in_=grouped[t][:])
+        def load_words(i):
+            src = W_qkv_words[:, :, 2 * E * i : 2 * E * (i + 1)].rearrange("g p n -> p g n")
+            nc.sync.dma_start(out=words[i][:].bitcast(I32), in_=src.bitcast(I32))
 
-            def order_columns(i):
-                for g in range(PASSES):
-                    nc.vector.tensor_copy(
-                        out=w_codes[i][:, g, :].bitcast(I32).rearrange("p (c h w) -> p c h w", c=CHUNKS, h=H),
-                        in_=words[i][:, g, :].bitcast(I32).rearrange("p (h c w) -> p c h w", c=CHUNKS, h=H),
-                    )
-                for g in range(PASSES):
-                    nc.vector.tensor_copy(
-                        out=w_scales[i][:, g, :].bitcast(I32).rearrange("p (c h w) -> p c h w", c=CHUNKS, h=H),
-                        in_=scale_rows[:, g, E * i : E * (i + 1)].bitcast(I32).rearrange("p (h c w) -> p c h w", c=CHUNKS, h=H),
-                    )
+        def order_columns(i, dest, src):
+            blocks, chunks = (1, CHUNKS) if i < 2 else (2, BANK)
+            dest = dest.bitcast(I32).rearrange("p g (b c h w) -> p g b c h w", b=blocks, c=chunks, h=H // blocks)
+            src = src.bitcast(I32).rearrange("p g (b h c w) -> p g b c h w", b=blocks, c=chunks, h=H // blocks)
+            for g in range(PASSES):
+                for b in range(blocks):
+                    nc.vector.tensor_copy(out=dest[:, g, b], in_=src[:, g, b])
 
-            soft = head.tile([P, 4, H], F32)
+        def order_weights(i):
+            order_columns(i, w_scales[i][:], scale_rows[:, :, E * i : E * (i + 1)])
+            order_columns(i, w_codes[i][:], words[i][:])
+
+        nc.vector.memset(scale_rows[:].bitcast(I32), 0)
+        nc.vector.memset(bias_rows[:], 0.0)
+        make_identity(nc, ident)
+        make_identity(nc, ident_bf[:])
+        nc.gpsimd.memset(kT[:, :, 0:K_PAD], 0.0)
+        nc.gpsimd.memset(vT[:, :, 0:V_PAD], 0.0)
+        nc.gpsimd.memset(by_key[:], 0.0)
+
+        load_x(0)
+        nc.sync.dma_start(out=bypass[:], in_=identity_bypass.partition_broadcast(P))
+        for quad in range(4):
+            src = W_qkv_scales[:, 4 * quad : 4 * quad + 4, :].rearrange("g r n -> r g n")
+            nc.sync.dma_start(out=scale_rows[32 * quad : 32 * quad + 4, :, :].bitcast(I32), in_=src.bitcast(I32))
+        for i in range(2):
+            nc.sync.dma_start(
+                out=bias_rows[CHUNKS * i : CHUNKS * (i + 1), :].rearrange("c (h l) -> c h l", h=H),
+                in_=b_qkv[E * i : E * (i + 1)].rearrange("(h c l) -> c h l", h=H, c=CHUNKS),
+            )
+        for b in range(2):
+            row, col = 2 * CHUNKS + BANK * b, 2 * E + b * E // 2
+            nc.sync.dma_start(
+                out=bias_rows[row : row + BANK, :].rearrange("c (h l) -> c h l", h=HALF),
+                in_=b_qkv[col : col + E // 2].rearrange("(h c l) -> c h l", h=HALF, c=BANK),
+            )
+        load_words(1)
+        load_words(0)
+        load_x(1)
+        load_words(2)
+        rows = H * TILES
+        all_gain_rows = gains[0].rearrange("h (t p) j -> (h t) (p j)", p=P)
+        nc.sync.dma_start(out=gain_rows[0][:], in_=all_gain_rows[0:P, :])
+        nc.sync.dma_start(out=gain_rows[1][:], in_=all_gain_rows[rows - P : rows, :])
+        nc.sync.dma_start(
+            out=pos[:].rearrange("p j a h -> p (j a h)"),
+            in_=pos_bias.rearrange("r h -> (r h)").partition_broadcast(P),
+        )
+        for q in range(4):
+            nc.sync.dma_start(out=scratch(q, PITCH)[:, :, ROW:PITCH], in_=by_key[:, 0:QUARTER, 0 : PITCH - ROW])
+
+        def local_gain():
             nc.scalar.activation(out=soft[:, 0, :], in_=bypass[:], func=ACT.Abs)
             nc.scalar.activation(out=soft[:, 1, :], in_=soft[:, 0, :], func=ACT.Exp, scale=-1.0)
             nc.scalar.activation(out=soft[:, 2, :], in_=soft[:, 1, :], func=ACT.Ln, bias=1.0)
             nc.scalar.activation(out=soft[:, 3, :], in_=bypass[:], func=ACT.Relu)
+            nc.gpsimd.tensor_tensor(out=tap_gain[:, 0, :], in0=soft[:, 2, :], in1=soft[:, 3, :], op=ALU.add)
 
-            turn_x(0)
-            bias_t = psum.tile([P, P], BF16, tag="w", name="bias_t")
-            nc.tensor.transpose(bias_t[:], bias_rows[:], ident_bf[:])
-            order_columns(0)
-            quantize_x(0)
-            order_columns(1)
-            nc.vector.tensor_copy(out=bias[:], in_=bias_t[:, 0 : 3 * CHUNKS])
-            nc.vector.tensor_tensor(out=tap_gain[:, 0, :], in0=soft[:, 2, :], in1=soft[:, 3, :], op=ALU.add)
-            turn_x(1)
-            for t in range(1, TILES):
-                if t + 1 < TILES:
-                    turn_x(t + 1)
-                quantize_x(t)
-            order_columns(2)
-            nc.vector.memset(tap_bias[:, 0, :], 0.0)
-            nc.vector.tensor_copy(out=tap_bias[:, 1:12, :], in_=pos[:, :, 0, :])
-            nc.vector.tensor_copy(out=tap_bias[:, 12:13, :], in_=pos[:, 0:1, 1, :])
-            nc.vector.tensor_copy(out=tap_bias[:, 13:32:2, :], in_=pos[:, 1:11, 1, :])
-            nc.vector.tensor_copy(out=tap_bias[:, 14:32:2, :], in_=pos[:, 0:9, 3, :])
-            nc.vector.tensor_copy(out=tap_bias[:, 32:42, :], in_=pos[:, 0:10, 2, :])
-            for i in range(2):
-                first = 0 if i == 0 else 2 * P - rows
-                for j0 in range(0, S, 8):
-                    count = min(8, S - j0)
-                    gain_t = psum.tile([P, 8, P], BF16, tag="w", name="gain_t")
-                    for j in range(count):
-                        nc.tensor.transpose(gain_t[:, j, :], gain_rows[i][:, j0 + j : P * S : S], ident_bf[:])
-                    nc.scalar.copy(
-                        out=gain[:, j0 : j0 + count, i * P : i * P + P - first], in_=gain_t[:, 0:count, first:P]
-                    )
+        def turn_bias():
+            bank = psum.tile([P, P], BF16, tag="s", name="bias_t")
+            nc.tensor.transpose(bank[:], bias_rows[:], ident_bf[:])
+            nc.vector.tensor_copy(out=bias[:], in_=bank[:, 0 : 3 * CHUNKS])
 
-        work = ctx.enter_context(tc.tile_pool(name="work", bufs=1))
+        def order_tap_bias():
+            nc.gpsimd.memset(tap_bias[:, 0, :], 0.0)
+            for tap_rows, tau, scales in TAP_RUNS:
+                nc.scalar.copy(out=tap_bias[:, tap_rows, :], in_=pos[:, scales, tau, :])
+            nc.scalar.copy(out=rotations[:, P : 2 * P - H], in_=rotations[:, 0 : P - H])
+
+        def turn_gains(i, j0):
+            first = 0 if i == 0 else 2 * P - rows
+            count = min(8, S - j0)
+            bank = psum.tile([P, 8, P], BF16, tag="w", name="gain_t")
+            for j in range(count):
+                nc.tensor.transpose(bank[:, j, :], gain_rows[i][:, j0 + j : P * S : S], ident_bf[:])
+            nc.scalar.copy(out=gain[:, j0 : j0 + count, i * P : i * P + P - first], in_=bank[:, 0:count, first:P])
+
         waiting = []
 
         def later(steps, call):
@@ -191,10 +225,14 @@ def tile_dwarfattention_pa_kernel(tc, x, W_qkv_words, W_qkv_scales, b_qkv, gains
         def step():
             for entry in waiting:
                 entry[0] -= 1
-            due = [entry for entry in waiting if entry[0] <= 0]
-            for entry in due:
+            for entry in [entry for entry in waiting if entry[0] <= 0]:
                 waiting.remove(entry)
                 entry[1]()
+
+
+        q_psum, q_sbuf, scores, weights, inverse, turned, spread = {}, {}, {}, {}, {}, {}, {}
+        parts, sums, pairs, v_rows, before, within, results = {}, {}, {}, {}, {}, {}, {}
+        unsummed, chain = [], {}
 
         def project(i, t, b, tag, dest):
             acc = psum.tile([P, BANK, P], F32, tag=tag, name="proj")
@@ -204,8 +242,8 @@ def tile_dwarfattention_pa_kernel(tc, x, W_qkv_words, W_qkv_scales, b_qkv, gains
                         out=acc[:, c % BANK, :],
                         lhsT=w_codes[i][:, g, 2 * P * c : 2 * P * (c + 1)].bitcast(E2M1X4),
                         lhsT_scale=w_scales[i][:, g, P * c : P * (c + 1)],
-                        rhs=x_codes[:, t, P * g : P * (g + 1)].bitcast(E5M2X4),
-                        rhs_scale=x_scales[:, t, P * g : P * (g + 1)],
+                        rhs=x_codes[t][:, P * g : P * (g + 1)].bitcast(E5M2X4),
+                        rhs_scale=x_scales[t][:, P * g : P * (g + 1)],
                         start=(g == 0),
                         stop=(g == PASSES - 1),
                     )
@@ -216,59 +254,49 @@ def tile_dwarfattention_pa_kernel(tc, x, W_qkv_words, W_qkv_scales, b_qkv, gains
                 )
             return acc
 
-        q_psum, q_sbuf, scores, weights, spread, turned, turned_sbuf = {}, {}, {}, {}, {}, {}, {}
+        def project_q(t):
+            q_sbuf[t] = work.tile([P, CHUNKS, P], F32, name="q_sbuf", bufs=2)
+            for b in range(2):
+                q_psum[t, b] = project(0, t, b, "q", q_sbuf[t])
 
-        def project_q(t, b):
-            if b == 0:
-                q_sbuf[t] = work.tile([P, CHUNKS, P], F32, name="q_sbuf", bufs=2)
-            q_psum[t, b] = project(0, t, b, "q", q_sbuf[t])
+        def project_k(t, b):
+            project(1, t, b, "w", kT[:, :, K_PAD + t * P : K_PAD + (t + 1) * P])
 
-        def project_k(t, b, tag):
-            project(1, t, b, tag, kT[:, :, PAD + t * P : PAD + (t + 1) * P])
-
-        def project_v(t, b, tag):
-            project(2, t, b, tag, vT[:, :, PAD + t * P : PAD + (t + 1) * P])
+        def project_v(t, b):
+            project(2, t, b, "w", vT[:, :, V_PAD + t * P : V_PAD + (t + 1) * P])
 
         def product_tile(gpsimd):
             if gpsimd:
                 return work.tile([P, CHUNKS, P], F32, name="product_g", bufs=3)
             return work.tile([P, CHUNKS, P], F32, name="product_v", bufs=4)
 
-        def window(t, s):
-            first = PAD + t * P - OFFSETS[s]
+        def window(t, s, pad):
+            first = pad + t * P - OFFSETS[s]
             return slice(first, first + P)
 
-        def gains_of_taps(t):
-            g = gain[:, :, t : H * TILES : TILES]
-            for tau, tap_rows, scales in (
-                (0, slice(1, 12), slice(0, 11)),
-                (1, slice(12, 13), slice(0, 1)),
-                (1, slice(13, 32, 2), slice(1, 11)),
-                (3, slice(14, 32, 2), slice(0, 9)),
-                (2, slice(32, 42), slice(0, 10)),
-            ):
-                nc.scalar.activation(out=tap_gain[:, tap_rows, :], in_=g[:, scales, :], func=ACT.Copy, scale=abs(D4[tau]))
+        def add_turned(dest, src, start, stop):
+            nc.tensor.matmul(dest, lhsT=src, rhs=ident, start=start, stop=stop, is_transpose=True)
 
-        def sum_lanes(t, group, part):
+        def sum_lanes(t, group):
+            if (t, group) not in unsummed:
+                return
+            unsummed.remove((t, group))
             nc.vector.tensor_reduce(
                 out=scores[t][:, group[0] : group[-1] + 1, :],
-                in_=part[:, 0 : len(group), :].rearrange("p s (h l) -> p s h l", l=LANES),
+                in_=parts[t, group[0] // BANK][:, 0 : len(group), :].rearrange("p s (h l) -> p s h l", l=LANES),
                 axis=AXIS.X,
                 op=ALU.add,
             )
 
-        parts, sums = {}, {}
-
-        def add_turned(dest, product, c, start, stop):
-            nc.tensor.matmul(dest, lhsT=product[:, c, :], rhs=ident[:], start=start, stop=stop, is_transpose=True)
-
         def score(t, s, gpsimd):
             group = slot_groups(t)[s // BANK]
             if s == group[0]:
+                if len(unsummed) == 2:
+                    sum_lanes(*unsummed[0])
                 parts[t, s // BANK] = psum.tile([P, BANK, P], F32, tag="s", name="part")
-            part = parts[t, s // BANK]
+            dest = parts[t, s // BANK][:, s % BANK, :]
             product = product_tile(gpsimd)
-            keys = kT[:, :, window(t, s)]
+            keys = kT[:, :, window(t, s, K_PAD)]
             if gpsimd:
                 nc.gpsimd.tensor_tensor(out=product[:], in0=q_sbuf[t][:], in1=keys, op=ALU.mult)
             else:
@@ -282,158 +310,320 @@ def tile_dwarfattention_pa_kernel(tc, x, W_qkv_words, W_qkv_scales, b_qkv, gains
                         op1=ALU.mult,
                     )
             for c in range(CHUNKS):
-                add_turned(part[:, s % BANK, :], product, c, c == 0, c == CHUNKS - 1)
+                add_turned(dest, product[:, c, :], c == 0, c == CHUNKS - 1)
             if s == group[-1]:
-                later(3, lambda: sum_lanes(t, group, part))
+                unsummed.append((t, group))
+                later(3, lambda: sum_lanes(t, group))
 
         def weight_steps(t):
-            u = work.tile([P, TAPS, H], F32, name="u")
-            low = work.tile([P, TAPS, H], F32, name="low")
-            high = work.tile([P, TAPS, H], F32, name="high")
-            zero_taps = work.tile([P, ZERO_TAPS, H], F32, name="zero_taps")
-            rest = work.tile([P, TAPS - ZERO_TAPS + 1, H], F32, name="rest")
-            z = work.tile([P, H], F32, name="z")
-            z_eps = work.tile([P, H], F32, name="z_eps")
-            inv = work.tile([P, H], F32, name="inv")
-            weights[t] = work.tile([P, SLOTS, H], F32, name="weights", bufs=2)
-            sc = scores[t]
+            near, far = t < TILES, t > 0
+            lo, hi = (0 if near else NEAR_TAPS), (TAPS if far else NEAR_TAPS)
+            tiles = {}
+
+            def gains_of_taps():
+                for tap_rows, tau, scales in TAP_RUNS:
+                    if lo <= tap_rows.start < hi:
+                        tile = t if tap_rows.start < NEAR_TAPS else t - 1
+                        g = gain[:, scales, tile : H * TILES : TILES]
+                        nc.scalar.activation(out=tap_gain[:, tap_rows, :], in_=g, func=ACT.Copy, scale=abs(D4[tau]))
 
             def add_bias():
-                nc.gpsimd.tensor_tensor(
-                    out=u[:, 0:12, :], in0=sc[:, 0:1, :].to_broadcast([P, 12, H]), in1=tap_bias[:, 0:12, :], op=ALU.add
-                )
-                nc.gpsimd.tensor_tensor(out=u[:, 12:32, :], in0=sc[:, 1:21, :], in1=tap_bias[:, 12:32, :], op=ALU.add)
-                nc.gpsimd.tensor_tensor(out=u[:, 32:42, :], in0=sc[:, 2:21:2, :], in1=tap_bias[:, 32:42, :], op=ALU.add)
-                nc.scalar.activation(out=low[:], in_=u[:], func=ACT.Relu, scale=-1.0)
-                nc.scalar.activation(out=low[:], in_=low[:], func=ACT.Exp, scale=-1.0)
-                nc.scalar.activation(out=high[:], in_=u[:], func=ACT.Relu)
+                u = tiles["u"] = work.tile([P, TAPS, H], F32, name="u")
+                low = tiles["low"] = work.tile([P, TAPS, H], F32, name="low")
+                runs = []
+                if near:
+                    runs.append((slice(0, 12), scores[t][:, 0:1, :].to_broadcast([P, ZERO_TAPS, H])))
+                    runs.append((slice(12, 26), scores[t][:, 1:NEAR, :]))
+                    runs.append((slice(26, 33), scores[t][:, 2:NEAR:2, :]))
+                if far:
+                    runs.append((slice(33, 36), scores[t - 1][:, NEAR + 1 : SLOTS : 2, :]))
+                    runs.append((slice(36, 42), scores[t - 1][:, NEAR:SLOTS, :]))
+                for tap_rows, src in runs:
+                    nc.gpsimd.tensor_tensor(out=u[:, tap_rows, :], in0=src, in1=tap_bias[:, tap_rows, :], op=ALU.add)
+                gains_of_taps()
+                nc.scalar.activation(out=low[:, lo:hi, :], in_=u[:, lo:hi, :], func=ACT.Relu, scale=-1.0)
+                nc.scalar.activation(out=low[:, lo:hi, :], in_=low[:, lo:hi, :], func=ACT.Exp, scale=-1.0)
+                nc.scalar.activation(out=u[:, lo:hi, :], in_=u[:, lo:hi, :], func=ACT.Relu)
 
             def weigh():
-                nc.gpsimd.tensor_tensor(out=u[:], in0=low[:], in1=high[:], op=ALU.add)
-                nc.gpsimd.tensor_tensor(out=zero_taps[:], in0=u[:, 0:12, :], in1=tap_gain[:, 0:12, :], op=ALU.mult)
-                nc.gpsimd.tensor_tensor(out=rest[:, 1:31, :], in0=u[:, 12:42, :], in1=tap_gain[:, 12:42, :], op=ALU.mult)
-                nc.gpsimd.tensor_tensor(out=rest[:, 2:21:2, :], in0=rest[:, 2:21:2, :], in1=rest[:, 21:31, :], op=ALU.add)
-
-            def sum_zero_taps():
-                nc.vector.tensor_reduce(
-                    out=rest[:, 0, :], in_=zero_taps[:].rearrange("p r h -> p h r"), axis=AXIS.X, op=ALU.add
+                u, low = tiles["u"], tiles["low"]
+                w = weights[t] = work.tile([P, NEAR_SUM_ROW + 1, H], F32, name="weights", bufs=2)
+                nc.gpsimd.tensor_tensor(out=u[:, lo:hi, :], in0=u[:, lo:hi, :], in1=low[:, lo:hi, :], op=ALU.add)
+                first = max(lo, ZERO_TAPS)
+                shift = ZERO_TAPS - 1
+                nc.gpsimd.tensor_tensor(
+                    out=w[:, first - shift : hi - shift, :], in0=u[:, first:hi, :], in1=tap_gain[:, first:hi, :], op=ALU.mult
                 )
+                if near:
+                    nc.gpsimd.tensor_tensor(
+                        out=low[:, 0:ZERO_TAPS, :], in0=u[:, 0:ZERO_TAPS, :], in1=tap_gain[:, 0:ZERO_TAPS, :], op=ALU.mult
+                    )
+                    nc.gpsimd.tensor_tensor(out=w[:, 2:NEAR:2, :], in0=w[:, 2:NEAR:2, :], in1=w[:, 15:22, :], op=ALU.add)
+                if far:
+                    nc.gpsimd.tensor_tensor(out=w[:, 26:31:2, :], in0=w[:, 26:31:2, :], in1=w[:, 22:25, :], op=ALU.add)
+
+            def sum_rows(dest, src):
+                nc.vector.tensor_reduce(out=dest, in_=src.rearrange("p r h -> p h r"), axis=AXIS.X, op=ALU.add)
+
+            def sum_taps():
+                if near:
+                    sum_rows(weights[t][:, 0, :], tiles["low"][:, 0:ZERO_TAPS, :])
+                if far:
+                    sum_rows(weights[t][:, NEAR_SUM_ROW, :], weights[t - 1][:, 0:NEAR, :])
 
             def sum_all():
-                nc.vector.tensor_reduce(
-                    out=z[:], in_=rest[:, 0:SLOTS, :].rearrange("p r h -> p h r"), axis=AXIS.X, op=ALU.add
-                )
-                nc.scalar.activation(out=z_eps[:], in_=z[:], func=ACT.Copy, bias=1e-06)
+                z = tiles["z"] = work.tile([P, 2, H], F32, name="z")
+                sum_rows(z[:, 0, :], weights[t][:, FAR_ROW : NEAR_SUM_ROW + 1, :])
+                nc.scalar.activation(out=z[:, 1, :], in_=z[:, 0, :], func=ACT.Copy, bias=1e-06)
 
             def invert():
-                nc.vector.reciprocal(out=inv[:], in_=z_eps[:])
+                inverse[t - 1] = work.tile([P, H], F32, name="inverse", bufs=2)
+                nc.vector.reciprocal(out=inverse[t - 1][:], in_=tiles["z"][:, 1, :])
 
-            def normalise():
-                nc.gpsimd.tensor_tensor(
-                    out=weights[t][:],
-                    in0=rest[:, 0:SLOTS, :],
-                    in1=inv[:].unsqueeze(1).to_broadcast([P, SLOTS, H]),
-                    op=ALU.mult,
+            return add_bias, weigh, sum_taps, sum_all, invert
+
+        def start_weights(t):
+            for entry in list(unsummed):
+                if entry[0] < t or entry[1][0] < NEAR:
+                    sum_lanes(*entry)
+            chain[t] = weight_steps(t)
+            chain[t][0]()
+
+        def by_chunk(bank):
+            return bank[:].rearrange("p (h c l) -> p c h l", h=HALF, c=BANK)
+
+        def turn_values(t, b):
+            if b == 0:
+                v_rows[t] = work.tile([P, E], F32, name="v_rows", bufs=2)
+            bank = psum.tile([P, E // 2], F32, tag="w", name="values")
+            for c in range(BANK):
+                src = vT[:, BANK * b + c, V_PAD + t * P : V_PAD + (t + 1) * P]
+                nc.tensor.transpose(by_chunk(bank)[:, c], src, ident)
+            nc.scalar.copy(out=v_rows[t][:, b * E // 2 : (b + 1) * E // 2], in_=bank[:])
+
+        def turn_near_weights(t):
+            bank = psum.tile([P, 2, P], F32, tag="w", name="near")
+            for g in range(2):
+                src = weights[t][:, CHUNKS * g : CHUNKS * (g + 1), :].rearrange("p s h -> p (s h)")
+                nc.tensor.transpose(bank[:, g, :], src, ident)
+            if t > 0:
+                nc.scalar.copy(out=pairs[t - 1][:, :, P : 2 * P], in_=bank[:])
+            pairs[t] = work.tile([P, 2, 2 * P], F32, name="pair", bufs=2)
+            nc.scalar.copy(out=pairs[t][:, :, 0:P], in_=bank[:])
+            if t == TILES - 1:
+                nc.gpsimd.memset(pairs[t][:, :, P : 2 * P], 0.0)
+
+        def index_by_key(t, rows_of_keys):
+            bank = psum.tile([P, BANK * P], F32, tag="w", name="keyed")
+            for s in range(NEAR):
+                src = pairs[t][:, s // CHUNKS, OFFSETS[s] : OFFSETS[s] + P]
+                turn = rotations[:, H * (s % CHUNKS) : H * (s % CHUNKS) + P]
+                nc.tensor.transpose(bank[:, H * s : H * s + P], src, turn)
+            keyed = bank[:, 0 : NEAR * H].rearrange("p (s h) -> p h s", h=H)
+            nc.scalar.copy(out=rows_of_keys[:, :, 0:3], in_=keyed[:, :, 0:3])
+            for s in range(3, NEAR - 2):
+                if s % 4 in (3, 0):
+                    lo, hi = OFFSETS[s], OFFSETS[s + 2]
+                    nc.scalar.activation(
+                        out=rows_of_keys[:, :, lo : hi + 1 : hi - lo],
+                        in_=keyed[:, :, s : s + 3 : 2],
+                        func=ACT.Copy,
+                        scale=-1.0 if s % 2 else 1.0,
+                    )
+
+        def park(q, rows_of_keys):
+            src = rows_of_keys[:, QUARTER * q : QUARTER * (q + 1), :]
+            nc.sync.dma_start(out=scratch(q, PITCH)[:, :, 0:ROW], in_=src)
+
+        def fetch(t, q):
+            skewed = scratch(q, PITCH - 1)
+            if t + 1 < TILES:
+                within[t, q] = work.tile([P, QUARTER, P], F32, name="within", bufs=4)
+            elif q % 2 == 0:
+                both = product_tile(True)
+                within[t, q], within[t, q + 1] = both[:, 0:QUARTER, :], both[:, QUARTER : 2 * QUARTER, :]
+            nc.sync.dma_start(out=within[t, q][:], in_=skewed[:, :, 0:P])
+            if t + 1 < TILES:
+                before[t + 1, q] = work.tile([P, QUARTER, P], F32, name="before", bufs=4)
+                nc.sync.dma_start(out=before[t + 1, q][:], in_=skewed[:, :, P : 2 * P])
+
+        def skew(t, rows_of_keys):
+            index_by_key(t, rows_of_keys)
+            for q in range(4):
+                park(q, rows_of_keys)
+            for q in range(4):
+                fetch(t, q)
+
+        def band(t, q, earlier):
+            opens = earlier or t == 0
+            if opens and q == 0:
+                sums[t] = [psum.tile([P, E // 2], F32, tag="acc", name="acc") for b in range(2)]
+            for h in range(QUARTER * q, QUARTER * (q + 1)):
+                nc.tensor.matmul(
+                    sums[t][h // HALF][:, HD * (h % HALF) : HD * (h % HALF + 1)],
+                    lhsT=(before if earlier else within)[t, q][:, h % QUARTER, :],
+                    rhs=v_rows[t - 1 if earlier else t][:, HD * h : HD * (h + 1)],
+                    start=(h % HALF == 0 and opens),
+                    stop=(h % HALF == HALF - 1 and not earlier),
                 )
-
-            return [(0.2, add_bias), (0.4, weigh), (0.65, sum_zero_taps), (0.7, sum_all), (0.75, invert), (0.95, normalise)]
 
         def spread_weights(t):
-            spread[t] = work.tile([P, SLOTS, H, LANES], F32, name="spread")
-            top = len(live_slots(t))
-            for slots, sign in ((slice(0, 2), 1.0), (slice(2, top, 2), 1.0), (slice(3, top, 2), -1.0)):
-                dest = spread[t][:, slots, :, :]
-                src = weights[t][:, slots, :].unsqueeze(3).to_broadcast(list(dest.shape))
-                nc.scalar.activation(out=dest, in_=src, func=ACT.Copy, scale=sign)
+            spread[t] = work.tile([P, FAR, H, V_LANES], F32, name="spread")
+            count = len(far_slots(t))
+            for first, sign in ((0, -1.0), (1, 1.0)):
+                if first < count:
+                    dest = spread[t][:, first:count:2, :, :]
+                    src = weights[t + 1][:, FAR_ROW + first : FAR_ROW + count : 2, :]
+                    nc.scalar.activation(
+                        out=dest, in_=src.unsqueeze(3).to_broadcast(list(dest.shape)), func=ACT.Copy, scale=sign
+                    )
 
-        def turn_weights(t, n, shared):
-            group = slot_groups(t)[n]
-            bank = psum.tile([P, BANK, P], F32, tag="w", name="turned")
-            for s in group:
-                nc.tensor.transpose(bank[:, s % BANK, :], spread[t][:, s, :, :].rearrange("p h l -> p (h l)"), ident[:])
-                turned[t, s] = bank[:, s % BANK : s % BANK + 1, :]
-            for s in group:
-                if s in shared:
-                    turned_sbuf[t, s] = work.tile([P, 1, P], F32, name="turned_sbuf", bufs=4)
-                    nc.scalar.copy(out=turned_sbuf[t, s][:], in_=turned[t, s])
+        def turn_far_weights(t, n):
+            bank = psum.tile([P, 2, 2, P], F32, tag="w", name="turned")
+            for s in far_slots(t)[2 * n : 2 * n + 2]:
+                for b in range(2):
+                    src = spread[t][:, s - NEAR, HALF * b : HALF * (b + 1), :].rearrange("p h l -> p (h l)")
+                    nc.tensor.transpose(bank[:, (s - NEAR) % 2, b, :], src, ident)
+                turned[t, s] = bank[:, (s - NEAR) % 2, :, :]
+
+        def weigh_values(t, s):
+            product = product_tile(False)
+            nc.vector.tensor_tensor(
+                out=product[:].rearrange("p (b c) n -> p b c n", b=2),
+                in0=vT[:, :, window(t, s, V_PAD)].rearrange("p (b c) n -> p b c n", b=2),
+                in1=turned[t, s].unsqueeze(2).to_broadcast([P, 2, BANK, P]),
+                op=ALU.mult,
+            )
+            for c in range(CHUNKS):
+                add_turned(by_chunk(sums[t][c // BANK])[:, c % BANK], product[:, c, :], False, False)
+            if s == NEAR + 1 and len(far_slots(t)) > 4:
+                turn_far_weights(t, 2)
+
+        def finish(t):
+            tag = "q_sbuf" if t in (TILES - 3, TILES - 2) else "result"
+            results[t] = work.tile([P, H, HD], F32, name="result", tag=tag, bufs=2)
+            for h in range(H):
+                nc.scalar.activation(
+                    out=results[t][:, h, :],
+                    in_=sums[t][h // HALF][:, HD * (h % HALF) : HD * (h % HALF + 1)],
+                    func=ACT.Copy,
+                    scale=inverse[t][:, h : h + 1],
+                )
 
         def store(t):
-            result = work.tile([P, H, CHUNKS, LANES], F32, name="result", bufs=2)
-            for b in range(2):
-                nc.scalar.copy(
-                    out=result[:, :, BANK * b : BANK * (b + 1), :],
-                    in_=sums[t][b][:].rearrange("p c (h l) -> p h c l", l=LANES),
-                )
-            nc.sync.dma_start(out=out[0, t * P : (t + 1) * P, :], in_=result[:].rearrange("p h c l -> p (h c l)"))
+            nc.sync.dma_start(out=out[0, t * P : (t + 1) * P, :], in_=results[t][:].rearrange("p h d -> p (h d)"))
 
-        def weigh_values(t, s, shared):
-            last = len(live_slots(t)) - 1
-            if s == 0:
-                sums[t] = [psum.tile([P, BANK, P], F32, tag="acc", name="acc") for b in range(2)]
-            product = product_tile(s in shared)
-            values = vT[:, :, window(t, s)]
-            if s in shared:
-                w = turned_sbuf[t, s][:].to_broadcast([P, CHUNKS, P])
-                nc.gpsimd.tensor_tensor(out=product[:], in0=values, in1=w, op=ALU.mult)
-            else:
-                w = turned[t, s].to_broadcast([P, CHUNKS, P])
-                nc.vector.tensor_tensor(out=product[:], in0=values, in1=w, op=ALU.mult)
-            for c in range(CHUNKS):
-                first, final = s == 0 and c % BANK == 0, s == last and c % BANK == BANK - 1
-                add_turned(sums[t][c // BANK][:, c % BANK, :], product, c, first, final)
-            if s % BANK == BANK - 1 and s // BANK + 2 <= last // BANK:
-                turn_weights(t, s // BANK + 2, shared)
-            if s == last:
+        def close_tile(t):
+            finish(t)
+            if t < first_parked_tile:
                 store(t)
 
-        for b in range(2):
-            project_q(0, b)
-            project_k(0, b, "s")
-        for period in range(TILES + LAG):
-            t, tw, tv = period, period - 1, period - LAG
-            n_score = len(live_slots(t)) if t < TILES else 0
-            n_value = len(live_slots(tv)) if tv >= 0 else 0
-            total = n_score + n_value
-            side = (n_score + BANK - 1) // BANK / 2 - (WEIGHT_WORK if 0 <= tw < TILES else 0)
-            n_gpsimd = round((total + side) / 3)
-            flags = [on_gpsimd(i, (n_gpsimd, total)) for i in range(total)]
-            n_vector_scores = n_score - n_gpsimd
-            shared = [i for i in range(total) if flags[i]] if n_score == 0 else []
-            if n_score:
-                scores[t] = work.tile([P, SLOTS, H], F32, name="scores", bufs=2)
-                if n_score < SLOTS:
-                    nc.gpsimd.memset(scores[t][:, n_score:SLOTS, :], 0.0)
-            if 0 <= tw < TILES:
-                later(1, lambda tw=tw: gains_of_taps(tw))
-                for place, call in weight_steps(tw):
-                    later(max(4, round(place * total)), call)
-            if n_value:
-                spread_weights(tv)
-                later(3 if n_score else 0, lambda tv=tv, shared=shared: turn_weights(tv, 0, shared))
-                later(5 if n_score else 0, lambda tv=tv, shared=shared: turn_weights(tv, 1, shared))
-                if not n_score:
-                    step()
-            if t + 1 < TILES and not n_value:
-                for b in range(2):
-                    later(2 + 2 * b, lambda t=t, b=b: project_k(t + 1, b, "w"))
-                    later(6 + 2 * b, lambda t=t, b=b: project_v(t, b, "w"))
-            next_score = next_value = vector_done = 0
-            for i in range(total):
-                if n_score and (flags[i] or vector_done < n_vector_scores):
-                    score(t, next_score, flags[i])
-                    next_score += 1
-                    vector_done += not flags[i]
-                    if vector_done == n_vector_scores and not flags[i]:
-                        if n_value:
-                            for b in range(2):
-                                later(1 + 2 * b, lambda t=t, b=b: project_v(t, b, "q"))
-                                if t + 1 < TILES:
-                                    later(5 + 2 * b, lambda t=t, b=b: project_k(t + 1, b, "q"))
-                                    later(9 + 2 * b, lambda t=t, b=b: project_q(t + 1, b))
-                        else:
-                            project_q(t + 1, 0)
-                            project_q(t + 1, 1)
-                else:
-                    weigh_values(tv, next_value, shared)
-                    next_value += 1
+        def jobs_of(t):
+            tw, tv, done = t - 1, t - LAG, t - LAG - 1
+            weigh, sum_taps, sum_all, invert = chain[tw][1:] if tw >= 0 else [None] * 4
+            far_pairs = min(2, (len(far_slots(tv)) + 1) // 2) if tv >= 0 else 0
+            jobs = [
+                [(t == 0, project_v, 0, 0), (done >= 0, band, done, 0, False)],
+                [(t == 0, project_v, 0, 1), (done >= 0, band, done, 1, False)],
+                [(t == 0, order_tap_bias), (done >= 0, band, done, 2, False)],
+                [(done >= 0, band, done, 3, False), (done >= 0, close_tile, done)],
+                [(t + 1 < TILES, project_k, t + 1, 0), (tw >= 0, weigh)],
+                [(t + 1 < TILES, project_k, t + 1, 1)],
+                [(t == 0, turn_gains, 0, 0), (tv >= 1, band, tv, 0, True)],
+                [(t == 0, turn_gains, 0, 8), (tv >= 1, band, tv, 1, True), (tw >= 0, sum_taps)],
+                [(t == 0, turn_gains, 1, 0), (tv >= 1, band, tv, 2, True), (tw >= 0, turn_near_weights, tw)],
+                [(t == 0, turn_gains, 1, 8), (tv >= 1, band, tv, 3, True), (tv >= 0, sum_all)],
+                [(tv >= 0, skew, tv, by_key)],
+                [(t + 2 < TILES, turn_x, t + 2), (far_pairs, spread_weights, tv)],
+                [(t + 1 < TILES, project_v, t + 1, 0), (tv >= 0, invert)],
+                [(t + 1 < TILES, project_v, t + 1, 1)],
+                [(tv >= 0, turn_values, tv, 0), (t + 2 < TILES, quantize_x, t + 2)],
+                [(tv >= 0, turn_values, tv, 1)],
+                [(far_pairs > 0, turn_far_weights, tv, 0)],
+                [(far_pairs > 1, turn_far_weights, tv, 1)],
+            ]
+            return [[call[1:] for call in job if call[0]] for job in jobs]
+
+        def run(job):
+            for call in job:
+                call[0](*call[1:])
+
+        local_gain()
+        turn_x(0)
+        turn_bias()
+        order_weights(1)
+        quantize_x(0)
+        order_weights(0)
+        project_k(0, 0)
+        project_k(0, 1)
+        turn_x(1)
+        project_q(0)
+        order_weights(2)
+        quantize_x(1)
+        for t in range(TILES):
+            tv = t - LAG
+            n_score = len(live_slots(t))
+            far = far_slots(tv) if tv >= 0 else []
+            side = (n_score + BANK - 1) // BANK / 2 - (WEIGHT_WORK if t else 0)
+            n_gpsimd = round((n_score + len(far) + side) / 3)
+            scores[t] = work.tile([P, SLOTS, H], F32, name="scores", bufs=2)
+            if n_score < SLOTS:
+                nc.gpsimd.memset(scores[t][:, n_score:SLOTS, :], 0.0)
+            if t + 2 < TILES:
+                load_x(t + 2)
+            jobs = jobs_of(t)
+            for i in range(n_score):
+                score(t, i, spread_evenly(i, n_gpsimd, n_score))
                 step()
+                for job in jobs[i * len(jobs) // n_score : (i + 1) * len(jobs) // n_score]:
+                    run(job)
+                if i == n_score - 2 and t + 1 < TILES:
+                    project_q(t + 1)
+            start_weights(t)
+            for s in far:
+                weigh_values(tv, s)
+                step()
+
+        last = TILES - 1
+        last_by_key = kT[:].rearrange("p c n -> p (c n)")[:, 0 : H * ROW].rearrange("p (h i) -> p h i", h=H)
+        weigh, sum_taps, sum_all, invert = chain[last][1:]
+        weigh()
+        for q in range(4):
+            band(last - 2, q, False)
+        close_tile(last - 2)
+        sum_taps()
+        turn_near_weights(last)
+        nc.gpsimd.memset(last_by_key, 0.0)
+        start_weights(TILES)
+        for q in range(4):
+            band(last - 1, q, True)
+        skew(last - 1, by_key)
+        skew(last, last_by_key)
+        for i in range(first_parked_tile, last - 1):
+            store(i)
+        sum_all()
+        spread_weights(last - 1)
+        for b in range(2):
+            turn_values(last - 1, b)
+        invert()
+        weigh, sum_taps, sum_all, invert = chain[TILES][1:]
+        weigh()
+        for t in (last - 1, last):
+            for n in range(2):
+                turn_far_weights(t, n)
+            for s in far_slots(t):
+                weigh_values(t, s)
+            if t < last:
+                sum_taps()
+                sum_all()
+                spread_weights(last)
+                invert()
+            for q in range(4):
+                band(t, q, False)
+            finish(t)
+            store(t)
+            if t < last:
+                for b in range(2):
+                    turn_values(last, b)
+                for q in range(4):
+                    band(last, q, True)

from contextlib import ExitStack

import concourse.mybir as mybir
from concourse.masks import make_identity

N, D, H, HD, S = 1536, 1024, 16, 64, 11
E = H * HD
D4 = [0.4829629131445341, 0.8365163037378079, 0.2241438680420134, -0.1294095225512604]
FLOPS = 2 * N * D * 3 * E

F32 = mybir.dt.float32
BF16 = mybir.dt.bfloat16
I32 = mybir.dt.int32
U32 = mybir.dt.uint32
U8 = mybir.dt.uint8
E5M2X4 = mybir.dt.float8_e5m2_x4
E2M1X4 = mybir.dt.float4_e2m1fn_x4
ALU = mybir.AluOpType
ACT = mybir.ActivationFunctionType
AXIS = mybir.AxisListType

P = 128
TILES = N // P
PASSES = D // 512
CHUNKS = 8
BANK = 4
LANES = HD // CHUNKS
V_LANES = HD // BANK
HALF = H // 2
QUARTER = H // 4
K_PAD = 96
V_PAD = 64
OFFSETS = sorted({(1 << j) * tau for j in range(S) for tau in range(4) if (1 << j) * tau < N})
SLOTS = len(OFFSETS)
NEAR = 15
FAR = SLOTS - NEAR
ROW = 136
PITCH = 264
HEAD_WORDS = P * PITCH
LAG = 2
WEIGHT_WORK = 6
PRESUM = 0

ZERO_TAPS = 1 + S
NEAR_TAPS = 33
TAPS = 42
TAP_RUNS = (
    (slice(1, 12), 0, slice(0, 11)),
    (slice(12, 13), 1, slice(0, 1)),
    (slice(13, 26, 2), 1, slice(1, 8)),
    (slice(14, 26, 2), 3, slice(0, 6)),
    (slice(26, 33), 2, slice(0, 7)),
    (slice(33, 36), 2, slice(7, 10)),
    (slice(36, 42, 2), 3, slice(6, 9)),
    (slice(37, 42, 2), 1, slice(8, 11)),
)
FAR_ROW = 25
NEAR_SUM_ROW = FAR_ROW + FAR


def live_slots(t):
    return [s for s in range(SLOTS) if OFFSETS[s] < P * (t + 1)]


def far_slots(t):
    return live_slots(t)[NEAR:]


def slot_groups(t):
    live = live_slots(t)
    return [live[i : i + BANK] for i in range(0, len(live), BANK)]


def spread_evenly(i, count, total):
    return (i + 1) * count // total > i * count // total


def tile_dwarfattention_pa_kernel(tc, x, W_qkv_words, W_qkv_scales, b_qkv, gains, pos_bias, identity_bypass, out):
    nc = tc.nc
    with ExitStack() as ctx:
        ctx.enter_context(tc.manual_schedule())
        keep = ctx.enter_context(tc.tile_pool(name="keep", bufs=1))
        work = ctx.enter_context(tc.tile_pool(name="work", bufs=1))
        psum = ctx.enter_context(tc.psum_pool(name="psum", bufs=2))

        rotations = keep.tile([P, 2 * P - H], F32)
        ident = rotations[:, 0:P]
        ident_bf = keep.tile([P, P], BF16)
        kT = keep.tile([P, CHUNKS, K_PAD + N], F32)
        vT = keep.tile([P, CHUNKS, V_PAD + N], F32)
        w_codes = [keep.tile([P, PASSES, 2 * E], U8, name="w_codes%d" % i, align_bytes=64) for i in range(3)]
        w_scales = [keep.tile([P, PASSES, E], U8, name="w_scales%d" % i, align_bytes=64) for i in range(3)]
        gain = keep.tile([P, S, H * TILES], BF16)
        bias = keep.tile([P, 3 * CHUNKS], F32)
        tap_bias = keep.tile([P, TAPS, H], BF16)
        tap_gain = keep.tile([P, TAPS, H], F32)
        by_key = keep.tile([P, H, ROW], F32)
        bias_rows = keep.tile([P, P], BF16)
        bypass = keep.tile([P, H], BF16)
        soft = keep.tile([P, 4, H], F32)

        flat_out = out.rearrange("b n e -> (b n e)")
        first_word = N * E - H * HEAD_WORDS
        first_parked_tile = first_word // (P * E)

        def scratch(q, pitch):
            lo = first_word + q * QUARTER * HEAD_WORDS
            heads = flat_out[lo : lo + QUARTER * HEAD_WORDS].rearrange("(h r) -> h r", h=QUARTER)
            return heads[:, 0 : P * pitch].rearrange("h (m i) -> m h i", i=pitch)

        x_rows, grouped, x_codes, x_scales = {}, {}, {}, {}

        def load_x(t):
            x_rows[t] = work.tile([P, D], BF16, name="x_rows", bufs=2)
            nc.sync.dma_start(out=x_rows[t][:], in_=x[0, t * P : (t + 1) * P, :])

        def turn_x(t):
            xt = psum.tile([P, PASSES, 2, P], F32, tag="w", name="xt")
            pairs_of_k = x_rows[t][:].bitcast(F32)
            for g in range(PASSES):
                for u in range(2):
                    nc.tensor.transpose(xt[:, g, u, :], pairs_of_k[:, 256 * g + u : 256 * (g + 1) : 2], ident)
            grouped[t] = work.tile([P, D], BF16, name="grouped", align_bytes=64)
            nc.scalar.copy(
                out=grouped[t][:].bitcast(F32).rearrange("p (g r u) -> p g r u", g=PASSES, u=2),
                in_=xt[:].rearrange("p g u r -> p g r u"),
            )

        def quantize_x(t):
            x_codes[t] = work.tile([P, PASSES * P], U32, name="x_codes", bufs=2, align_bytes=64)
            x_scales[t] = work.tile([P, PASSES * P], U8, name="x_scales", bufs=2, align_bytes=64)
            nc.vector.quantize_mx(out=x_codes[t][:].bitcast(E5M2X4), scales=x_scales[t][:], in_=grouped[t][:])

        scale_rows = work.tile([P, PASSES, 3 * E], U8, tag="spread")
        words = [work.tile([P, PASSES, 2 * E], U8, name="words", tag=tag, bufs=2) for tag in ("result", "result", "v_rows")]
        gain_rows = [work.tile([P, P * S], BF16, name="gain_rows", tag=tag) for tag in ("u", "low")]
        pos = work.tile([P, S, 4, H], BF16, tag="weights", bufs=2)

        def load_words(i):
            src = W_qkv_words[:, :, 2 * E * i : 2 * E * (i + 1)].rearrange("g p n -> p g n")
            nc.sync.dma_start(out=words[i][:].bitcast(I32), in_=src.bitcast(I32))

        def order_columns(i, dest, src):
            blocks, chunks = (1, CHUNKS) if i < 2 else (2, BANK)
            dest = dest.bitcast(I32).rearrange("p g (b c h w) -> p g b c h w", b=blocks, c=chunks, h=H // blocks)
            src = src.bitcast(I32).rearrange("p g (b h c w) -> p g b c h w", b=blocks, c=chunks, h=H // blocks)
            for g in range(PASSES):
                for b in range(blocks):
                    nc.vector.tensor_copy(out=dest[:, g, b], in_=src[:, g, b])

        def order_weights(i):
            order_columns(i, w_scales[i][:], scale_rows[:, :, E * i : E * (i + 1)])
            order_columns(i, w_codes[i][:], words[i][:])

        nc.vector.memset(scale_rows[:].bitcast(I32), 0)
        nc.vector.memset(bias_rows[:], 0.0)
        make_identity(nc, ident)
        make_identity(nc, ident_bf[:])
        nc.gpsimd.memset(kT[:, :, 0:K_PAD], 0.0)
        nc.gpsimd.memset(vT[:, :, 0:V_PAD], 0.0)
        nc.gpsimd.memset(by_key[:], 0.0)

        load_x(0)
        nc.sync.dma_start(out=bypass[:], in_=identity_bypass.partition_broadcast(P))
        for quad in range(4):
            src = W_qkv_scales[:, 4 * quad : 4 * quad + 4, :].rearrange("g r n -> r g n")
            nc.sync.dma_start(out=scale_rows[32 * quad : 32 * quad + 4, :, :].bitcast(I32), in_=src.bitcast(I32))
        for i in range(2):
            nc.sync.dma_start(
                out=bias_rows[CHUNKS * i : CHUNKS * (i + 1), :].rearrange("c (h l) -> c h l", h=H),
                in_=b_qkv[E * i : E * (i + 1)].rearrange("(h c l) -> c h l", h=H, c=CHUNKS),
            )
        for b in range(2):
            row, col = 2 * CHUNKS + BANK * b, 2 * E + b * E // 2
            nc.sync.dma_start(
                out=bias_rows[row : row + BANK, :].rearrange("c (h l) -> c h l", h=HALF),
                in_=b_qkv[col : col + E // 2].rearrange("(h c l) -> c h l", h=HALF, c=BANK),
            )
        load_words(1)
        load_words(0)
        load_x(1)
        load_words(2)
        rows = H * TILES
        all_gain_rows = gains[0].rearrange("h (t p) j -> (h t) (p j)", p=P)
        nc.sync.dma_start(out=gain_rows[0][:], in_=all_gain_rows[0:P, :])
        nc.sync.dma_start(out=gain_rows[1][:], in_=all_gain_rows[rows - P : rows, :])
        nc.sync.dma_start(
            out=pos[:].rearrange("p j a h -> p (j a h)"),
            in_=pos_bias.rearrange("r h -> (r h)").partition_broadcast(P),
        )
        for q in range(4):
            nc.sync.dma_start(out=scratch(q, PITCH)[:, :, ROW:PITCH], in_=by_key[:, 0:QUARTER, 0 : PITCH - ROW])

        def local_gain():
            nc.scalar.activation(out=soft[:, 0, :], in_=bypass[:], func=ACT.Abs)
            nc.scalar.activation(out=soft[:, 1, :], in_=soft[:, 0, :], func=ACT.Exp, scale=-1.0)
            nc.scalar.activation(out=soft[:, 2, :], in_=soft[:, 1, :], func=ACT.Ln, bias=1.0)
            nc.scalar.activation(out=soft[:, 3, :], in_=bypass[:], func=ACT.Relu)
            nc.gpsimd.tensor_tensor(out=tap_gain[:, 0, :], in0=soft[:, 2, :], in1=soft[:, 3, :], op=ALU.add)

        def turn_bias():
            bank = psum.tile([P, P], BF16, tag="s", name="bias_t")
            nc.tensor.transpose(bank[:], bias_rows[:], ident_bf[:])
            nc.vector.tensor_copy(out=bias[:], in_=bank[:, 0 : 3 * CHUNKS])

        def order_tap_bias():
            nc.gpsimd.memset(tap_bias[:, 0, :], 0.0)
            for tap_rows, tau, scales in TAP_RUNS:
                nc.scalar.copy(out=tap_bias[:, tap_rows, :], in_=pos[:, scales, tau, :])
            nc.scalar.copy(out=rotations[:, P : 2 * P - H], in_=rotations[:, 0 : P - H])

        def turn_gains(i, j0):
            first = 0 if i == 0 else 2 * P - rows
            count = min(8, S - j0)
            bank = psum.tile([P, 8, P], BF16, tag="w", name="gain_t")
            for j in range(count):
                nc.tensor.transpose(bank[:, j, :], gain_rows[i][:, j0 + j : P * S : S], ident_bf[:])
            nc.scalar.copy(out=gain[:, j0 : j0 + count, i * P : i * P + P - first], in_=bank[:, 0:count, first:P])

        waiting = []

        def later(steps, call):
            waiting.append([steps, call])

        def step():
            for entry in waiting:
                entry[0] -= 1
            for entry in [entry for entry in waiting if entry[0] <= 0]:
                waiting.remove(entry)
                entry[1]()


        q_psum, q_sbuf, scores, weights, inverse, turned, spread = {}, {}, {}, {}, {}, {}, {}
        parts, sums, pairs, v_rows, before, within, results = {}, {}, {}, {}, {}, {}, {}
        unsummed, chain = [], {}

        def project(i, t, b, tag, dest):
            acc = psum.tile([P, BANK, P], F32, tag=tag, name="proj")
            for c in range(BANK * b, BANK * (b + 1)):
                for g in range(PASSES):
                    nc.tensor.matmul_mx(
                        out=acc[:, c % BANK, :],
                        lhsT=w_codes[i][:, g, 2 * P * c : 2 * P * (c + 1)].bitcast(E2M1X4),
                        lhsT_scale=w_scales[i][:, g, P * c : P * (c + 1)],
                        rhs=x_codes[t][:, P * g : P * (g + 1)].bitcast(E5M2X4),
                        rhs_scale=x_scales[t][:, P * g : P * (g + 1)],
                        start=(g == 0),
                        stop=(g == PASSES - 1),
                    )
            for c in range(BANK * b, BANK * (b + 1)):
                col = CHUNKS * i + c
                nc.scalar.activation(
                    out=dest[:, c, :], in_=acc[:, c % BANK, :], func=ACT.Identity, bias=bias[:, col : col + 1]
                )
            return acc

        def project_q(t):
            q_sbuf[t] = work.tile([P, CHUNKS, P], F32, name="q_sbuf", bufs=2)
            for b in range(2):
                q_psum[t, b] = project(0, t, b, "q", q_sbuf[t])

        def project_k(t, b):
            project(1, t, b, "w", kT[:, :, K_PAD + t * P : K_PAD + (t + 1) * P])

        def project_v(t, b):
            project(2, t, b, "w", vT[:, :, V_PAD + t * P : V_PAD + (t + 1) * P])

        def product_tile(gpsimd):
            if gpsimd:
                return work.tile([P, CHUNKS, P], F32, name="product_g", bufs=3)
            return work.tile([P, CHUNKS, P], F32, name="product_v", bufs=4)

        def window(t, s, pad):
            first = pad + t * P - OFFSETS[s]
            return slice(first, first + P)

        def add_turned(dest, src, start, stop):
            nc.tensor.matmul(dest, lhsT=src, rhs=ident, start=start, stop=stop, is_transpose=True)

        def sum_lanes(t, group):
            if (t, group) not in unsummed:
                return
            unsummed.remove((t, group))
            nc.vector.tensor_reduce(
                out=scores[t][:, group[0] : group[-1] + 1, :],
                in_=parts[t, group[0] // BANK][:, 0 : len(group), :].rearrange("p s (h l) -> p s h l", l=LANES),
                axis=AXIS.X,
                op=ALU.add,
            )

        def score(t, s, gpsimd):
            group = slot_groups(t)[s // BANK]
            if s == group[0]:
                if len(unsummed) == 2:
                    sum_lanes(*unsummed[0])
                parts[t, s // BANK] = psum.tile([P, BANK, P], F32, tag="s", name="part")
            dest = parts[t, s // BANK][:, s % BANK, :]
            product = product_tile(gpsimd)
            keys = kT[:, :, window(t, s, K_PAD)]
            if gpsimd:
                nc.gpsimd.tensor_tensor(out=product[:], in0=q_sbuf[t][:], in1=keys, op=ALU.mult)
            else:
                for c in range(CHUNKS):
                    nc.vector.scalar_tensor_tensor(
                        out=product[:, c, :],
                        in0=q_psum[t, c // BANK][:, c % BANK, :],
                        scalar=bias[:, c : c + 1],
                        in1=keys[:, c, :],
                        op0=ALU.add,
                        op1=ALU.mult,
                    )
            for c in range(CHUNKS):
                add_turned(dest, product[:, c, :], c == 0, c == CHUNKS - 1)
            if s == group[-1]:
                unsummed.append((t, group))
                later(3, lambda: sum_lanes(t, group))

        def weight_steps(t):
            near, far = t < TILES, t > 0
            lo, hi = (0 if near else NEAR_TAPS), (TAPS if far else NEAR_TAPS)
            tiles = {}

            def gains_of_taps():
                for tap_rows, tau, scales in TAP_RUNS:
                    if lo <= tap_rows.start < hi:
                        tile = t if tap_rows.start < NEAR_TAPS else t - 1
                        g = gain[:, scales, tile : H * TILES : TILES]
                        nc.scalar.activation(out=tap_gain[:, tap_rows, :], in_=g, func=ACT.Copy, scale=abs(D4[tau]))

            def add_bias():
                u = tiles["u"] = work.tile([P, TAPS, H], F32, name="u")
                low = tiles["low"] = work.tile([P, TAPS, H], F32, name="low")
                runs = []
                if near:
                    runs.append((slice(0, 12), scores[t][:, 0:1, :].to_broadcast([P, ZERO_TAPS, H])))
                    runs.append((slice(12, 26), scores[t][:, 1:NEAR, :]))
                    runs.append((slice(26, 33), scores[t][:, 2:NEAR:2, :]))
                if far:
                    runs.append((slice(33, 36), scores[t - 1][:, NEAR + 1 : SLOTS : 2, :]))
                    runs.append((slice(36, 42), scores[t - 1][:, NEAR:SLOTS, :]))
                for tap_rows, src in runs:
                    nc.gpsimd.tensor_tensor(out=u[:, tap_rows, :], in0=src, in1=tap_bias[:, tap_rows, :], op=ALU.add)
                gains_of_taps()
                nc.scalar.activation(out=low[:, lo:hi, :], in_=u[:, lo:hi, :], func=ACT.Relu, scale=-1.0)
                nc.scalar.activation(out=low[:, lo:hi, :], in_=low[:, lo:hi, :], func=ACT.Exp, scale=-1.0)
                nc.scalar.activation(out=u[:, lo:hi, :], in_=u[:, lo:hi, :], func=ACT.Relu)

            def weigh():
                u, low = tiles["u"], tiles["low"]
                w = weights[t] = work.tile([P, NEAR_SUM_ROW + 1, H], F32, name="weights", bufs=2)
                nc.gpsimd.tensor_tensor(out=u[:, lo:hi, :], in0=u[:, lo:hi, :], in1=low[:, lo:hi, :], op=ALU.add)
                first = max(lo, ZERO_TAPS)
                shift = ZERO_TAPS - 1
                nc.gpsimd.tensor_tensor(
                    out=w[:, first - shift : hi - shift, :], in0=u[:, first:hi, :], in1=tap_gain[:, first:hi, :], op=ALU.mult
                )
                if near:
                    nc.gpsimd.tensor_tensor(
                        out=low[:, 0:ZERO_TAPS, :], in0=u[:, 0:ZERO_TAPS, :], in1=tap_gain[:, 0:ZERO_TAPS, :], op=ALU.mult
                    )
                    nc.gpsimd.tensor_tensor(out=w[:, 2:NEAR:2, :], in0=w[:, 2:NEAR:2, :], in1=w[:, 15:22, :], op=ALU.add)
                if far:
                    nc.gpsimd.tensor_tensor(out=w[:, 26:31:2, :], in0=w[:, 26:31:2, :], in1=w[:, 22:25, :], op=ALU.add)

            def sum_rows(dest, src):
                nc.vector.tensor_reduce(out=dest, in_=src.rearrange("p r h -> p h r"), axis=AXIS.X, op=ALU.add)

            def sum_taps():
                if near:
                    sum_rows(weights[t][:, 0, :], tiles["low"][:, 0:ZERO_TAPS, :])
                if far:
                    sum_rows(weights[t][:, NEAR_SUM_ROW, :], weights[t - 1][:, 0:NEAR, :])

            def sum_all():
                z = tiles["z"] = work.tile([P, 2, H], F32, name="z")
                sum_rows(z[:, 0, :], weights[t][:, FAR_ROW : NEAR_SUM_ROW + 1, :])
                nc.scalar.activation(out=z[:, 1, :], in_=z[:, 0, :], func=ACT.Copy, bias=1e-06)

            def invert():
                inverse[t - 1] = work.tile([P, H], F32, name="inverse", bufs=2)
                nc.vector.reciprocal(out=inverse[t - 1][:], in_=tiles["z"][:, 1, :])

            return add_bias, weigh, sum_taps, sum_all, invert

        def start_weights(t):
            for entry in list(unsummed):
                if entry[0] < t or entry[1][0] < NEAR:
                    sum_lanes(*entry)
            chain[t] = weight_steps(t)
            chain[t][0]()

        def by_chunk(bank):
            return bank[:].rearrange("p (h c l) -> p c h l", h=HALF, c=BANK)

        def turn_values(t, b):
            if b == 0:
                v_rows[t] = work.tile([P, E], F32, name="v_rows", bufs=2)
            bank = psum.tile([P, E // 2], F32, tag="w", name="values")
            for c in range(BANK):
                src = vT[:, BANK * b + c, V_PAD + t * P : V_PAD + (t + 1) * P]
                nc.tensor.transpose(by_chunk(bank)[:, c], src, ident)
            nc.scalar.copy(out=v_rows[t][:, b * E // 2 : (b + 1) * E // 2], in_=bank[:])

        def turn_near_weights(t):
            bank = psum.tile([P, 2, P], F32, tag="w", name="near")
            for g in range(2):
                src = weights[t][:, CHUNKS * g : CHUNKS * (g + 1), :].rearrange("p s h -> p (s h)")
                nc.tensor.transpose(bank[:, g, :], src, ident)
            if t > 0:
                nc.scalar.copy(out=pairs[t - 1][:, :, P : 2 * P], in_=bank[:])
            pairs[t] = work.tile([P, 2, 2 * P], F32, name="pair", bufs=2)
            nc.scalar.copy(out=pairs[t][:, :, 0:P], in_=bank[:])
            if t == TILES - 1:
                nc.gpsimd.memset(pairs[t][:, :, P : 2 * P], 0.0)

        def index_by_key(t, rows_of_keys):
            bank = psum.tile([P, BANK * P], F32, tag="w", name="keyed")
            for s in range(NEAR):
                src = pairs[t][:, s // CHUNKS, OFFSETS[s] : OFFSETS[s] + P]
                turn = rotations[:, H * (s % CHUNKS) : H * (s % CHUNKS) + P]
                nc.tensor.transpose(bank[:, H * s : H * s + P], src, turn)
            keyed = bank[:, 0 : NEAR * H].rearrange("p (s h) -> p h s", h=H)
            nc.scalar.copy(out=rows_of_keys[:, :, 0:3], in_=keyed[:, :, 0:3])
            for s in range(3, NEAR - 2):
                if s % 4 in (3, 0):
                    lo, hi = OFFSETS[s], OFFSETS[s + 2]
                    nc.scalar.activation(
                        out=rows_of_keys[:, :, lo : hi + 1 : hi - lo],
                        in_=keyed[:, :, s : s + 3 : 2],
                        func=ACT.Copy,
                        scale=-1.0 if s % 2 else 1.0,
                    )

        def park(q, rows_of_keys):
            src = rows_of_keys[:, QUARTER * q : QUARTER * (q + 1), :]
            nc.sync.dma_start(out=scratch(q, PITCH)[:, :, 0:ROW], in_=src)

        def fetch(t, q):
            skewed = scratch(q, PITCH - 1)
            if t + 1 < TILES:
                within[t, q] = work.tile([P, QUARTER, P], F32, name="within", bufs=4)
            elif q % 2 == 0:
                both = product_tile(True)
                within[t, q], within[t, q + 1] = both[:, 0:QUARTER, :], both[:, QUARTER : 2 * QUARTER, :]
            nc.sync.dma_start(out=within[t, q][:], in_=skewed[:, :, 0:P])
            if t + 1 < TILES:
                before[t + 1, q] = work.tile([P, QUARTER, P], F32, name="before", bufs=4)
                nc.sync.dma_start(out=before[t + 1, q][:], in_=skewed[:, :, P : 2 * P])

        def skew(t, rows_of_keys):
            index_by_key(t, rows_of_keys)
            for q in range(4):
                park(q, rows_of_keys)
            for q in range(4):
                fetch(t, q)

        def band(t, q, earlier):
            opens = earlier or t == 0
            if opens and q == 0:
                sums[t] = [psum.tile([P, E // 2], F32, tag="acc", name="acc") for b in range(2)]
            for h in range(QUARTER * q, QUARTER * (q + 1)):
                nc.tensor.matmul(
                    sums[t][h // HALF][:, HD * (h % HALF) : HD * (h % HALF + 1)],
                    lhsT=(before if earlier else within)[t, q][:, h % QUARTER, :],
                    rhs=v_rows[t - 1 if earlier else t][:, HD * h : HD * (h + 1)],
                    start=(h % HALF == 0 and opens),
                    stop=(h % HALF == HALF - 1 and not earlier),
                )

        def spread_weights(t):
            spread[t] = work.tile([P, FAR, H, V_LANES], F32, name="spread")
            count = len(far_slots(t))
            for first, sign in ((0, -1.0), (1, 1.0)):
                if first < count:
                    dest = spread[t][:, first:count:2, :, :]
                    src = weights[t + 1][:, FAR_ROW + first : FAR_ROW + count : 2, :]
                    nc.scalar.activation(
                        out=dest, in_=src.unsqueeze(3).to_broadcast(list(dest.shape)), func=ACT.Copy, scale=sign
                    )

        def turn_far_weights(t, n):
            bank = psum.tile([P, 2, 2, P], F32, tag="w", name="turned")
            for s in far_slots(t)[2 * n : 2 * n + 2]:
                for b in range(2):
                    src = spread[t][:, s - NEAR, HALF * b : HALF * (b + 1), :].rearrange("p h l -> p (h l)")
                    nc.tensor.transpose(bank[:, (s - NEAR) % 2, b, :], src, ident)
                turned[t, s] = bank[:, (s - NEAR) % 2, :, :]

        def weigh_values(t, s):
            product = product_tile(False)
            nc.vector.tensor_tensor(
                out=product[:].rearrange("p (b c) n -> p b c n", b=2),
                in0=vT[:, :, window(t, s, V_PAD)].rearrange("p (b c) n -> p b c n", b=2),
                in1=turned[t, s].unsqueeze(2).to_broadcast([P, 2, BANK, P]),
                op=ALU.mult,
            )
            for c in range(CHUNKS):
                add_turned(by_chunk(sums[t][c // BANK])[:, c % BANK], product[:, c, :], False, False)
            if s == NEAR + 1 and len(far_slots(t)) > 4:
                turn_far_weights(t, 2)

        def finish(t):
            tag = "q_sbuf" if t in (TILES - 3, TILES - 2) else "result"
            results[t] = work.tile([P, H, HD], F32, name="result", tag=tag, bufs=2)
            for h in range(H):
                nc.scalar.activation(
                    out=results[t][:, h, :],
                    in_=sums[t][h // HALF][:, HD * (h % HALF) : HD * (h % HALF + 1)],
                    func=ACT.Copy,
                    scale=inverse[t][:, h : h + 1],
                )

        def store(t):
            nc.sync.dma_start(out=out[0, t * P : (t + 1) * P, :], in_=results[t][:].rearrange("p h d -> p (h d)"))

        def close_tile(t):
            finish(t)
            if t < first_parked_tile:
                store(t)

        def jobs_of(t):
            tw, tv, done = t - 1, t - LAG, t - LAG - 1
            weigh, sum_taps, sum_all, invert = chain[tw][1:] if tw >= 0 else [None] * 4
            far_pairs = min(2, (len(far_slots(tv)) + 1) // 2) if tv >= 0 else 0
            jobs = [
                [(t == 0, project_v, 0, 0), (done >= 0, band, done, 0, False)],
                [(t == 0, project_v, 0, 1), (done >= 0, band, done, 1, False)],
                [(t == 0, order_tap_bias), (done >= 0, band, done, 2, False)],
                [(done >= 0, band, done, 3, False), (done >= 0, close_tile, done)],
                [(t + 1 < TILES, project_k, t + 1, 0), (tw >= 0, weigh)],
                [(t + 1 < TILES, project_k, t + 1, 1)],
                [(t == 0, turn_gains, 0, 0), (tv >= 1, band, tv, 0, True)],
                [(t == 0, turn_gains, 0, 8), (tv >= 1, band, tv, 1, True), (tw >= 0, sum_taps)],
                [(t == 0, turn_gains, 1, 0), (tv >= 1, band, tv, 2, True), (tw >= 0, turn_near_weights, tw)],
                [(t == 0, turn_gains, 1, 8), (tv >= 1, band, tv, 3, True), (tv >= 0, sum_all)],
                [(tv >= 0, skew, tv, by_key)],
                [(t + 2 < TILES, turn_x, t + 2), (far_pairs, spread_weights, tv)],
                [(t + 1 < TILES, project_v, t + 1, 0), (tv >= 0, invert)],
                [(t + 1 < TILES, project_v, t + 1, 1)],
                [(tv >= 0, turn_values, tv, 0), (t + 2 < TILES, quantize_x, t + 2)],
                [(tv >= 0, turn_values, tv, 1)],
                [(far_pairs > 0, turn_far_weights, tv, 0)],
                [(far_pairs > 1, turn_far_weights, tv, 1)],
            ]
            return [[call[1:] for call in job if call[0]] for job in jobs]

        def run(job):
            for call in job:
                call[0](*call[1:])

        local_gain()
        turn_x(0)
        turn_bias()
        order_weights(1)
        quantize_x(0)
        order_weights(0)
        project_k(0, 0)
        project_k(0, 1)
        turn_x(1)
        project_q(0)
        order_weights(2)
        quantize_x(1)
        for t in range(TILES):
            tv = t - LAG
            n_score = len(live_slots(t))
            far = far_slots(tv) if tv >= 0 else []
            side = (n_score + BANK - 1) // BANK / 2 - (WEIGHT_WORK if t else 0)
            n_gpsimd = round((n_score + len(far) + side) / 3)
            scores[t] = work.tile([P, SLOTS, H], F32, name="scores", bufs=2)
            if n_score < SLOTS:
                nc.gpsimd.memset(scores[t][:, n_score:SLOTS, :], 0.0)
            if t + 2 < TILES:
                load_x(t + 2)
            jobs = jobs_of(t)
            for i in range(n_score):
                score(t, i, spread_evenly(i, n_gpsimd, n_score))
                step()
                for job in jobs[i * len(jobs) // n_score : (i + 1) * len(jobs) // n_score]:
                    run(job)
                if i == n_score - 2 and t + 1 < TILES:
                    project_q(t + 1)
            start_weights(t)
            for s in far:
                weigh_values(tv, s)
                step()

        last = TILES - 1
        last_by_key = kT[:].rearrange("p c n -> p (c n)")[:, 0 : H * ROW].rearrange("p (h i) -> p h i", h=H)
        weigh, sum_taps, sum_all, invert = chain[last][1:]
        weigh()
        for q in range(4):
            band(last - 2, q, False)
        close_tile(last - 2)
        sum_taps()
        turn_near_weights(last)
        nc.gpsimd.memset(last_by_key, 0.0)
        start_weights(TILES)
        for q in range(4):
            band(last - 1, q, True)
        skew(last - 1, by_key)
        skew(last, last_by_key)
        for i in range(first_parked_tile, last - 1):
            store(i)
        sum_all()
        spread_weights(last - 1)
        for b in range(2):
            turn_values(last - 1, b)
        invert()
        weigh, sum_taps, sum_all, invert = chain[TILES][1:]
        weigh()
        for t in (last - 1, last):
            for n in range(2):
                turn_far_weights(t, n)
            for s in far_slots(t):
                weigh_values(t, s)
            if t < last:
                sum_taps()
                sum_all()
                spread_weights(last)
                invert()
            for q in range(4):
                band(t, q, False)
            finish(t)
            store(t)
            if t < last:
                for b in range(2):
                    turn_values(last, b)
                for q in range(4):
                    band(last, q, True)
